import numpy as np
import ml_dtypes


def mxq(x, axis, fmt="e4m3"):
    dtype, down = {"e4m3": (ml_dtypes.float8_e4m3fn, 7), "e5m2": (ml_dtypes.float8_e5m2, 14)}[fmt]
    v = np.moveaxis(np.asarray(x, np.float32).astype(ml_dtypes.bfloat16).astype(np.float64), axis, -1)
    blocks = v.reshape(v.shape[:-1] + (-1, 32))
    amax = np.abs(blocks).max(-1, keepdims=True)
    byte = np.maximum(np.where(amax > 0, np.frexp(amax)[1] - 1 + 127, 0) - down, 1)
    scale = np.exp2(byte - 127.0)
    codes = (blocks / scale).astype(np.float32).astype(dtype).astype(np.float64)
    return np.moveaxis((codes * scale).reshape(v.shape), -1, axis)


WIDE = False


def mx_kscale(k):
    if not WIDE:
        return np.ones(k)
    levels = np.array([10, -10, 5, -5, 0])
    a = np.random.permutation(np.resize(levels, k // 512 * 4)).reshape(k // 512, 4)
    idx = np.arange(k)
    return np.exp2(a[idx // 512, idx % 128 // 32])


BF16 = ml_dtypes.bfloat16


def bf(x):
    return np.asarray(x, np.float32).astype(BF16)


def f64(x):
    return np.asarray(x).astype(np.float64)


E2M1 = np.array([0.0, 0.5, 1.0, 1.5, 2.0, 3.0, 4.0, 6.0, -0.0, -0.5, -1.0, -1.5, -2.0, -3.0, -4.0, -6.0])


def pack_weight(w, fmt):
    k, n = w.shape
    w = f64(bf(w)).reshape(k // 32, 32, n)
    amax = np.abs(w).max(1)
    if fmt == "e4m3":
        byte = np.frexp(amax)[1] - 1 + 127 - 7
    else:
        mant, ex = np.frexp(amax / 6.0)
        byte = np.where(mant > 0.5, ex, ex - 1) + 127
    byte = np.clip(np.where(amax > 0, byte, 1), 1, 254)
    scaled = (w * np.exp2(127.0 - byte)[:, None, :]).reshape(k, n).astype(np.float32)
    by_word = np.ascontiguousarray(scaled.reshape(k // 512, 128, 4, n).transpose(0, 1, 3, 2))
    if fmt == "e4m3":
        words = by_word.astype(ml_dtypes.float8_e4m3fn).view(np.uint8)
    else:
        c = by_word.astype(ml_dtypes.float4_e2m1fn).view(np.uint8) & 0xF
        words = c[..., 0::2] | (c[..., 1::2] << 4)
    return np.ascontiguousarray(words), np.ascontiguousarray(byte.astype(np.uint8).reshape(k // 512, 16, n))


def unpack_weight(words, scales, fmt):
    g, p, n, _ = words.shape
    if fmt == "e4m3":
        vals = np.ascontiguousarray(words).view(ml_dtypes.float8_e4m3fn).astype(np.float64)
    else:
        nib = np.empty((g, p, n, 4), np.uint8)
        nib[..., 0::2] = words & 0xF
        nib[..., 1::2] = words >> 4
        vals = E2M1[nib]
    vals = vals * np.repeat(np.exp2(scales.astype(np.float64) - 127.0), 8, axis=1)[..., None]
    return vals.transpose(0, 1, 3, 2).reshape(g * 512, n)


B, F, E, H, D0, D1 = 1024, 16, 128, 128, 64, 128
FH = F * H


def setup_inputs():
    t = mx_kscale(FH)
    tf = t.reshape(F, H)
    x = bf(np.random.standard_normal((B, F, E)))
    feat_w = bf(np.random.standard_normal((F, E, H)) / np.sqrt(E) * tf[:, None, :])
    feat_b = bf(np.random.standard_normal((F, H)) * 0.2 * tf)
    trans_w_words, trans_w_scales = pack_weight(np.random.standard_normal((FH, FH)) / np.sqrt(FH) / t[:, None] * t[None, :], "e4m3")
    trans_b = bf(np.random.standard_normal(FH) * 0.2 * t)
    return {"x": x,
            "feat_w": feat_w,
            "feat_b": feat_b,
            "trans_w_words": trans_w_words,
            "trans_w_scales": trans_w_scales,
            "trans_b": trans_b}


def reference(x, feat_w, feat_b, trans_w_words, trans_w_scales, trans_b):
    pre = (f64(x).transpose(1, 0, 2) @ f64(feat_w)).transpose(1, 0, 2) + f64(feat_b)
    h = np.maximum(pre, 0.0)
    hf = h.reshape(B, FH)
    return np.maximum((mxq(hf, 1, "e4m3") @ unpack_weight(trans_w_words, trans_w_scales, "e4m3")) + f64(trans_b), 0.0) + hf

@@ -1,0 +1,188 @@
+from contextlib import ExitStack
+
+import concourse.mybir as mybir
+from concourse.masks import make_identity
+
+BF16 = mybir.dt.bfloat16
+F32 = mybir.dt.float32
+I32 = mybir.dt.int32
+U32 = mybir.dt.uint32
+U8 = mybir.dt.uint8
+FP8X4 = mybir.dt.float8_e4m3fn_x4
+ADD = mybir.AluOpType.add
+MAX = mybir.AluOpType.max
+RELU = mybir.ActivationFunctionType.Relu
+
+P = 128
+BATCH, FEATURES, E, H = 1024, 16, 128, 128
+K = FEATURES * H
+PACK = 4
+K_PASS = P * PACK
+PASSES = K // K_PASS
+FEATURES_PER_PASS = K_PASS // H
+BANK = 512
+COLUMN_BLOCKS = K // BANK
+ROW_BLOCKS = BATCH // P
+PLANE_STEP = 4
+QUADRANT = 32
+POOL_COLUMN_BLOCKS = 2
+
+FLOPS = 2 * BATCH * FEATURES * E * H + 2 * BATCH * K * K
+
+
+def tile_dsfs_pa_kernel(tc, x, feat_w, feat_b, trans_w_words, trans_w_scales, trans_b, out):
+    nc = tc.nc
+    with ExitStack() as stack:
+        keep = stack.enter_context(tc.tile_pool(name="keep", bufs=1))
+        pair = stack.enter_context(tc.tile_pool(name="pair", bufs=2))
+        triple = stack.enter_context(tc.tile_pool(name="triple", bufs=3))
+        results = stack.enter_context(tc.tile_pool(name="results", bufs=2 * COLUMN_BLOCKS))
+        psum_t = stack.enter_context(tc.psum_pool(name="psum_t", bufs=3))
+        psum_sum = stack.enter_context(tc.psum_pool(name="psum_sum", bufs=5))
+        stack.enter_context(tc.manual_schedule())
+
+        ident_bf16 = keep.tile([P, P], BF16)
+        make_identity(nc, ident_bf16[:])
+        ident_f32 = keep.tile([P, P], F32)
+        make_identity(nc, ident_f32[:])
+
+        bias_rows = keep.tile([P, 2, K], BF16)
+        nc.vector.memset(bias_rows[:].rearrange("p i k -> p (i k)").bitcast(I32), 0)
+        ones = keep.tile([P, P], BF16)
+        nc.vector.memset(ones[:], 1.0)
+        nc.scalar.dma_start(out=bias_rows[0:1, 0, :], in_=feat_b.rearrange("f h -> (f h)").unsqueeze(0))
+        nc.scalar.dma_start(out=bias_rows[0:1, 1, :], in_=trans_b.unsqueeze(0))
+
+        w_planes = keep.tile([P, K], U8, align_bytes=64)
+        nc.vector.memset(w_planes[:].bitcast(I32), 0)
+
+        x_rows = x.rearrange("b f e -> b (f e)")
+        x_blocks = [keep.tile([P, K], BF16, name="x_block%d" % r) for r in range(ROW_BLOCKS)]
+        feat_w_sb = keep.tile([E, FEATURES, H], BF16)
+        w_words = keep.tile([P, PASSES, K * PACK], U8, align_bytes=64)
+        w_words_dram = trans_w_words.rearrange("g p n t -> p g (n t)")
+
+        def load_x(r):
+            nc.sync.dma_start(out=x_blocks[r][:], in_=x_rows[r * P : (r + 1) * P, :])
+
+        def load_w(c):
+            some = slice(c * BANK * PACK, (c + 1) * BANK * PACK)
+            nc.sync.dma_start(out=w_words[:, :, some].bitcast(I32), in_=w_words_dram[:, :, some].bitcast(I32))
+
+        load_x(0)
+        nc.sync.dma_start(out=feat_w_sb[:], in_=feat_w.rearrange("f e h -> e f h"))
+        load_x(1)
+        for quadrant in range(P // QUADRANT):
+            first = quadrant * QUADRANT
+            nc.sync.dma_start(
+                out=w_planes[first : first + PASSES * PLANE_STEP, :].bitcast(I32),
+                in_=trans_w_scales[:, 4 * quadrant : 4 * quadrant + 4, :].bitcast(I32),
+            )
+        load_w(0)
+        load_x(2)
+        for c in range(1, COLUMN_BLOCKS):
+            load_w(c)
+        for r in range(3, ROW_BLOCKS):
+            load_x(r)
+
+        def spread_bias(i):
+            bias_all = keep.tile([P, K], BF16, name="bias_all%d" % i)
+            for c in range(COLUMN_BLOCKS):
+                cols = slice(c * BANK, (c + 1) * BANK)
+                repeated = psum_sum.tile([P, BANK], F32, tag="sum")
+                nc.tensor.matmul(out=repeated[:], lhsT=ones[:], rhs=bias_rows[:, i, cols], start=True, stop=True)
+                nc.scalar.copy(out=bias_all[:, cols], in_=repeated[:])
+            return bias_all
+
+        def transpose_x(r):
+            x_t = triple.tile([E, FEATURES, P], BF16)
+            per_bank = 2 * BANK // P
+            for first in range(0, FEATURES, per_bank):
+                turned = psum_t.tile([E, per_bank, P], BF16, tag="turned")
+                for j in range(per_bank):
+                    f = first + j
+                    nc.tensor.transpose(out=turned[:, j, :], in_=x_blocks[r][:, f * E : (f + 1) * E], identity=ident_bf16[:])
+                nc.scalar.copy(out=x_t[:, first : first + per_bank, :], in_=turned[:])
+            return x_t
+
+        def feature_layers(x_t, feat_b_all):
+            h_f32 = triple.tile([P, K], F32)
+            h_sorted = pair.tile([P, K], BF16)
+            for g in range(PASSES):
+                cols = slice(g * K_PASS, (g + 1) * K_PASS)
+                products = psum_sum.tile([P, K_PASS], F32, tag="sum")
+                for j in range(FEATURES_PER_PASS):
+                    f = g * FEATURES_PER_PASS + j
+                    nc.tensor.matmul(
+                        out=products[:, j * H : (j + 1) * H], lhsT=x_t[:, f, :], rhs=feat_w_sb[:, f, :], start=True, stop=True
+                    )
+                nc.vector.tensor_tensor(out=h_f32[:, cols], in0=products[:], in1=feat_b_all[:, cols], op=ADD)
+                nc.scalar.activation(
+                    out=h_sorted[:, cols].rearrange("b (u p e) -> b u p e", u=2, e=2),
+                    in_=h_f32[:, cols].rearrange("b (p u e) -> b u p e", u=2, e=2),
+                    func=RELU,
+                )
+            nc.gpsimd.tensor_scalar(out=h_f32[:], in0=h_f32[:], scalar1=0.0, scalar2=0.0, op0=MAX, op1=ADD)
+            return h_f32, h_sorted
+
+        def transpose_h(h_sorted):
+            h_words = h_sorted[:].bitcast(F32)
+            grouped = pair.tile([P, K], BF16, align_bytes=64)
+            grouped_words = grouped[:].bitcast(F32)
+            per_bank = BANK // (2 * P)
+            for first in range(0, PASSES, per_bank):
+                turned = psum_t.tile([P, per_bank, 2, P], F32, tag="turned")
+                for j in range(per_bank):
+                    for u in range(2):
+                        start = ((first + j) * 2 + u) * P
+                        nc.tensor.transpose(out=turned[:, j, u, :], in_=h_words[:, start : start + P], identity=ident_f32[:])
+                nc.scalar.copy(
+                    out=grouped_words[:, first * 2 * P : (first + per_bank) * 2 * P].rearrange(
+                        "p (g b u) -> p g b u", g=per_bank, u=2
+                    ),
+                    in_=turned[:].rearrange("p g u b -> p g b u"),
+                )
+            h_codes = pair.tile([P, PASSES * P], U32, align_bytes=64)
+            h_plane = pair.tile([P, PASSES * P], U8, align_bytes=64)
+            nc.vector.quantize_mx(out=h_codes[:].bitcast(FP8X4), scales=h_plane[:], in_=grouped[:])
+            return h_codes, h_plane
+
+        def big_matmul(r, h_codes, h_plane, h_f32, trans_b_all):
+            for c in range(COLUMN_BLOCKS):
+                cols = slice(c * BANK, (c + 1) * BANK)
+                sums = psum_sum.tile([P, BANK], F32, tag="sum")
+                for g in range(PASSES):
+                    rows_of_g = slice(g * P, (g + 1) * P)
+                    nc.tensor.matmul_mx(
+                        out=sums[:],
+                        lhsT=h_codes[:, rows_of_g].bitcast(FP8X4),
+                        lhsT_scale=h_plane[:, rows_of_g],
+                        rhs=w_words[:, g, c * BANK * PACK : (c + 1) * BANK * PACK].bitcast(FP8X4),
+                        rhs_scale=w_planes[g * PLANE_STEP : P, cols],
+                        start=(g == 0),
+                        stop=(g == PASSES - 1),
+                    )
+                result = results.tile([P, BANK], F32)
+                nc.vector.tensor_tensor(out=result[:], in0=sums[:], in1=trans_b_all[:, cols], op=ADD)
+                if c < POOL_COLUMN_BLOCKS:
+                    nc.scalar.activation(out=result[:], in_=result[:], func=RELU)
+                    nc.gpsimd.tensor_tensor(out=result[:], in0=result[:], in1=h_f32[:, cols], op=ADD)
+                else:
+                    nc.vector.scalar_tensor_tensor(
+                        out=result[:], in0=result[:], scalar=0.0, in1=h_f32[:, cols], op0=MAX, op1=ADD
+                    )
+                nc.sync.dma_start(out=out[r * P : (r + 1) * P, cols], in_=result[:])
+
+        turned_x = {0: transpose_x(0)}
+        feat_b_all = spread_bias(0)
+        layers = {0: feature_layers(turned_x[0], feat_b_all)}
+        turned_x[1] = transpose_x(1)
+        trans_b_all = spread_bias(1)
+        for r in range(ROW_BLOCKS):
+            h_f32, h_sorted = layers[r]
+            h_codes, h_plane = transpose_h(h_sorted)
+            if r + 2 < ROW_BLOCKS:
+                turned_x[r + 2] = transpose_x(r + 2)
+            if r + 1 < ROW_BLOCKS:
+                layers[r + 1] = feature_layers(turned_x[r + 1], feat_b_all)
+            big_matmul(r, h_codes, h_plane, h_f32, trans_b_all)

@@ -25,7 +25,6 @@ COLUMN_BLOCKS = K // BANK
 ROW_BLOCKS = BATCH // P
 PLANE_STEP = 4
 QUADRANT = 32
-POOL_COLUMN_BLOCKS = 2
 
 FLOPS = 2 * BATCH * FEATURES * E * H + 2 * BATCH * K * K
 
@@ -122,7 +121,7 @@ def tile_dsfs_pa_kernel(tc, x, feat_w, feat_b, trans_w_words, trans_w_scales, tr
                     in_=h_f32[:, cols].rearrange("b (p u e) -> b u p e", u=2, e=2),
                     func=RELU,
                 )
-            nc.gpsimd.tensor_scalar(out=h_f32[:], in0=h_f32[:], scalar1=0.0, scalar2=0.0, op0=MAX, op1=ADD)
+            nc.scalar.activation(out=h_f32[:], in_=h_f32[:], func=RELU)
             return h_f32, h_sorted
 
         def transpose_h(h_sorted):
@@ -164,13 +163,9 @@ def tile_dsfs_pa_kernel(tc, x, feat_w, feat_b, trans_w_words, trans_w_scales, tr
                     )
                 result = results.tile([P, BANK], F32)
                 nc.vector.tensor_tensor(out=result[:], in0=sums[:], in1=trans_b_all[:, cols], op=ADD)
-                if c < POOL_COLUMN_BLOCKS:
-                    nc.scalar.activation(out=result[:], in_=result[:], func=RELU)
-                    nc.gpsimd.tensor_tensor(out=result[:], in0=result[:], in1=h_f32[:, cols], op=ADD)
-                else:
-                    nc.vector.scalar_tensor_tensor(
-                        out=result[:], in0=result[:], scalar=0.0, in1=h_f32[:, cols], op0=MAX, op1=ADD
-                    )
+                nc.vector.scalar_tensor_tensor(
+                    out=result[:], in0=result[:], scalar=0.0, in1=h_f32[:, cols], op0=MAX, op1=ADD
+                )
                 nc.sync.dma_start(out=out[r * P : (r + 1) * P, cols], in_=result[:])
 
         turned_x = {0: transpose_x(0)}

@@ -35,6 +35,7 @@ def tile_dsfs_pa_kernel(tc, x, feat_w, feat_b, trans_w_words, trans_w_scales, tr
         keep = stack.enter_context(tc.tile_pool(name="keep", bufs=1))
         pair = stack.enter_context(tc.tile_pool(name="pair", bufs=2))
         triple = stack.enter_context(tc.tile_pool(name="triple", bufs=3))
+        quad = stack.enter_context(tc.tile_pool(name="quad", bufs=4))
         results = stack.enter_context(tc.tile_pool(name="results", bufs=2 * COLUMN_BLOCKS))
         psum_t = stack.enter_context(tc.psum_pool(name="psum_t", bufs=3))
         psum_sum = stack.enter_context(tc.psum_pool(name="psum_sum", bufs=5))
@@ -71,6 +72,7 @@ def tile_dsfs_pa_kernel(tc, x, feat_w, feat_b, trans_w_words, trans_w_scales, tr
         load_x(0)
         nc.sync.dma_start(out=feat_w_sb[:], in_=feat_w.rearrange("f e h -> e f h"))
         load_x(1)
+        load_x(2)
         for quadrant in range(P // QUADRANT):
             first = quadrant * QUADRANT
             nc.sync.dma_start(
@@ -78,10 +80,10 @@ def tile_dsfs_pa_kernel(tc, x, feat_w, feat_b, trans_w_words, trans_w_scales, tr
                 in_=trans_w_scales[:, 4 * quadrant : 4 * quadrant + 4, :].bitcast(I32),
             )
         load_w(0)
-        load_x(2)
+        load_x(3)
         for c in range(1, COLUMN_BLOCKS):
             load_w(c)
-        for r in range(3, ROW_BLOCKS):
+        for r in range(4, ROW_BLOCKS):
             load_x(r)
 
         def spread_bias(i):
@@ -90,7 +92,7 @@ def tile_dsfs_pa_kernel(tc, x, feat_w, feat_b, trans_w_words, trans_w_scales, tr
                 cols = slice(c * BANK, (c + 1) * BANK)
                 repeated = psum_sum.tile([P, BANK], F32, tag="sum")
                 nc.tensor.matmul(out=repeated[:], lhsT=ones[:], rhs=bias_rows[:, i, cols], start=True, stop=True)
-                nc.scalar.copy(out=bias_all[:, cols], in_=repeated[:])
+                nc.vector.tensor_copy(out=bias_all[:, cols], in_=repeated[:])
             return bias_all
 
         def transpose_x(r):
@@ -104,25 +106,29 @@ def tile_dsfs_pa_kernel(tc, x, feat_w, feat_b, trans_w_words, trans_w_scales, tr
                 nc.scalar.copy(out=x_t[:, first : first + per_bank, :], in_=turned[:])
             return x_t
 
-        def feature_layers(x_t, feat_b_all):
-            h_f32 = triple.tile([P, K], F32)
-            h_sorted = pair.tile([P, K], BF16)
-            for g in range(PASSES):
-                cols = slice(g * K_PASS, (g + 1) * K_PASS)
-                products = psum_sum.tile([P, K_PASS], F32, tag="sum")
-                for j in range(FEATURES_PER_PASS):
-                    f = g * FEATURES_PER_PASS + j
-                    nc.tensor.matmul(
-                        out=products[:, j * H : (j + 1) * H], lhsT=x_t[:, f, :], rhs=feat_w_sb[:, f, :], start=True, stop=True
-                    )
-                nc.vector.tensor_tensor(out=h_f32[:, cols], in0=products[:], in1=feat_b_all[:, cols], op=ADD)
-                nc.scalar.activation(
-                    out=h_sorted[:, cols].rearrange("b (u p e) -> b u p e", u=2, e=2),
-                    in_=h_f32[:, cols].rearrange("b (p u e) -> b u p e", u=2, e=2),
-                    func=RELU,
-                )
-            nc.scalar.activation(out=h_f32[:], in_=h_f32[:], func=RELU)
+        def feature_tiles():
+            h_f32 = quad.tile([P, K], F32)
+            h_sorted = triple.tile([P, K], BF16)
             return h_f32, h_sorted
+
+        def feature_pass(g, x_t, feat_b_all, h_f32, h_sorted):
+            cols = slice(g * K_PASS, (g + 1) * K_PASS)
+            products = psum_sum.tile([P, K_PASS], F32, tag="sum")
+            for j in range(FEATURES_PER_PASS):
+                f = g * FEATURES_PER_PASS + j
+                nc.tensor.matmul(
+                    out=products[:, j * H : (j + 1) * H], lhsT=x_t[:, f, :], rhs=feat_w_sb[:, f, :], start=True, stop=True
+                )
+            nc.vector.tensor_tensor(out=h_f32[:, cols], in0=products[:], in1=feat_b_all[:, cols], op=ADD)
+            nc.scalar.activation(
+                out=h_sorted[:, cols].rearrange("b (u p e) -> b u p e", u=2, e=2),
+                in_=h_f32[:, cols].rearrange("b (p u e) -> b u p e", u=2, e=2),
+                func=RELU,
+            )
+
+        def residual_relu(g, h_f32):
+            cols = slice(g * K_PASS, (g + 1) * K_PASS)
+            nc.scalar.activation(out=h_f32[:, cols], in_=h_f32[:, cols], func=RELU)
 
         def transpose_h(h_sorted):
             h_words = h_sorted[:].bitcast(F32)
@@ -141,12 +147,20 @@ def tile_dsfs_pa_kernel(tc, x, feat_w, feat_b, trans_w_words, trans_w_scales, tr
                     ),
                     in_=turned[:].rearrange("p g u b -> p g b u"),
                 )
-            h_codes = pair.tile([P, PASSES * P], U32, align_bytes=64)
-            h_plane = pair.tile([P, PASSES * P], U8, align_bytes=64)
+            h_codes = triple.tile([P, PASSES * P], U32, align_bytes=64)
+            h_plane = triple.tile([P, PASSES * P], U8, align_bytes=64)
             nc.vector.quantize_mx(out=h_codes[:].bitcast(FP8X4), scales=h_plane[:], in_=grouped[:])
             return h_codes, h_plane
 
         def big_matmul(r, h_codes, h_plane, h_f32, trans_b_all):
+            def finish(c, result):
+                cols = slice(c * BANK, (c + 1) * BANK)
+                nc.vector.scalar_tensor_tensor(
+                    out=result[:], in0=result[:], scalar=0.0, in1=h_f32[:, cols], op0=MAX, op1=ADD
+                )
+                nc.sync.dma_start(out=out[r * P : (r + 1) * P, cols], in_=result[:])
+
+            waiting = None
             for c in range(COLUMN_BLOCKS):
                 cols = slice(c * BANK, (c + 1) * BANK)
                 sums = psum_sum.tile([P, BANK], F32, tag="sum")
@@ -163,21 +177,35 @@ def tile_dsfs_pa_kernel(tc, x, feat_w, feat_b, trans_w_words, trans_w_scales, tr
                     )
                 result = results.tile([P, BANK], F32)
                 nc.vector.tensor_tensor(out=result[:], in0=sums[:], in1=trans_b_all[:, cols], op=ADD)
-                nc.vector.scalar_tensor_tensor(
-                    out=result[:], in0=result[:], scalar=0.0, in1=h_f32[:, cols], op0=MAX, op1=ADD
-                )
-                nc.sync.dma_start(out=out[r * P : (r + 1) * P, cols], in_=result[:])
+                if waiting is not None:
+                    finish(c - 1, waiting)
+                waiting = result
+            finish(COLUMN_BLOCKS - 1, waiting)
 
-        turned_x = {0: transpose_x(0)}
+        turned_x = {}
+        layers = {}
+        quantised = {}
+        turned_x[0] = transpose_x(0)
         feat_b_all = spread_bias(0)
-        layers = {0: feature_layers(turned_x[0], feat_b_all)}
         turned_x[1] = transpose_x(1)
+        layers[0] = feature_tiles()
+        for g in range(PASSES):
+            feature_pass(g, turned_x[0], feat_b_all, *layers[0])
+        turned_x[2] = transpose_x(2)
+        layers[1] = feature_tiles()
+        for g in range(PASSES):
+            feature_pass(g, turned_x[1], feat_b_all, *layers[1])
         trans_b_all = spread_bias(1)
+        quantised[0] = transpose_h(layers[0][1])
         for r in range(ROW_BLOCKS):
-            h_f32, h_sorted = layers[r]
-            h_codes, h_plane = transpose_h(h_sorted)
-            if r + 2 < ROW_BLOCKS:
-                turned_x[r + 2] = transpose_x(r + 2)
             if r + 1 < ROW_BLOCKS:
-                layers[r + 1] = feature_layers(turned_x[r + 1], feat_b_all)
-            big_matmul(r, h_codes, h_plane, h_f32, trans_b_all)
+                quantised[r + 1] = transpose_h(layers[r + 1][1])
+            if r + 3 < ROW_BLOCKS:
+                turned_x[r + 3] = transpose_x(r + 3)
+            if r + 2 < ROW_BLOCKS:
+                layers[r + 2] = feature_tiles()
+            for g in range(PASSES):
+                if r + 2 < ROW_BLOCKS:
+                    feature_pass(g, turned_x[r + 2], feat_b_all, *layers[r + 2])
+                residual_relu(g, layers[r][0])
+            big_matmul(r, *quantised[r], layers[r][0], trans_b_all)

@@ -147,6 +147,9 @@ def tile_dsfs_pa_kernel(tc, x, feat_w, feat_b, trans_w_words, trans_w_scales, tr
                     ),
                     in_=turned[:].rearrange("p g u b -> p g b u"),
                 )
+            return grouped
+
+        def quantise_h(grouped):
             h_codes = triple.tile([P, PASSES * P], U32, align_bytes=64)
             h_plane = triple.tile([P, PASSES * P], U8, align_bytes=64)
             nc.vector.quantize_mx(out=h_codes[:].bitcast(FP8X4), scales=h_plane[:], in_=grouped[:])
@@ -196,16 +199,20 @@ def tile_dsfs_pa_kernel(tc, x, feat_w, feat_b, trans_w_words, trans_w_scales, tr
         for g in range(PASSES):
             feature_pass(g, turned_x[1], feat_b_all, *layers[1])
         trans_b_all = spread_bias(1)
-        quantised[0] = transpose_h(layers[0][1])
+        quantised[0] = quantise_h(transpose_h(layers[0][1]))
         for r in range(ROW_BLOCKS):
             if r + 1 < ROW_BLOCKS:
-                quantised[r + 1] = transpose_h(layers[r + 1][1])
+                grouped_next = transpose_h(layers[r + 1][1])
             if r + 3 < ROW_BLOCKS:
                 turned_x[r + 3] = transpose_x(r + 3)
+            for g in range(PASSES // 2):
+                residual_relu(g, layers[r][0])
             if r + 2 < ROW_BLOCKS:
                 layers[r + 2] = feature_tiles()
-            for g in range(PASSES):
-                if r + 2 < ROW_BLOCKS:
+                for g in range(PASSES):
                     feature_pass(g, turned_x[r + 2], feat_b_all, *layers[r + 2])
+            if r + 1 < ROW_BLOCKS:
+                quantised[r + 1] = quantise_h(grouped_next)
+            for g in range(PASSES // 2, PASSES):
                 residual_relu(g, layers[r][0])
             big_matmul(r, *quantised[r], layers[r][0], trans_b_all)

@@ -37,8 +37,8 @@ def tile_dsfs_pa_kernel(tc, x, feat_w, feat_b, trans_w_words, trans_w_scales, tr
         triple = stack.enter_context(tc.tile_pool(name="triple", bufs=3))
         quad = stack.enter_context(tc.tile_pool(name="quad", bufs=4))
         results = stack.enter_context(tc.tile_pool(name="results", bufs=2 * COLUMN_BLOCKS))
-        psum_t = stack.enter_context(tc.psum_pool(name="psum_t", bufs=3))
-        psum_sum = stack.enter_context(tc.psum_pool(name="psum_sum", bufs=5))
+        psum_t = stack.enter_context(tc.psum_pool(name="psum_t", bufs=4))
+        psum_sum = stack.enter_context(tc.psum_pool(name="psum_sum", bufs=4))
         stack.enter_context(tc.manual_schedule())
 
         ident_bf16 = keep.tile([P, P], BF16)
@@ -46,12 +46,14 @@ def tile_dsfs_pa_kernel(tc, x, feat_w, feat_b, trans_w_words, trans_w_scales, tr
         ident_f32 = keep.tile([P, P], F32)
         make_identity(nc, ident_f32[:])
 
-        bias_rows = keep.tile([P, 2, K], BF16)
-        nc.vector.memset(bias_rows[:].rearrange("p i k -> p (i k)").bitcast(I32), 0)
+        feat_b_row = keep.tile([P, K], BF16)
+        nc.vector.memset(feat_b_row[:].bitcast(I32), 0)
+        nc.scalar.dma_start(out=feat_b_row[0:1, :], in_=feat_b.rearrange("f h -> (f h)").unsqueeze(0))
         ones = keep.tile([P, P], BF16)
         nc.vector.memset(ones[:], 1.0)
-        nc.scalar.dma_start(out=bias_rows[0:1, 0, :], in_=feat_b.rearrange("f h -> (f h)").unsqueeze(0))
-        nc.scalar.dma_start(out=bias_rows[0:1, 1, :], in_=trans_b.unsqueeze(0))
+        trans_b_row = keep.tile([P, K], BF16)
+        nc.vector.memset(trans_b_row[:].bitcast(I32), 0)
+        nc.scalar.dma_start(out=trans_b_row[0:1, :], in_=trans_b.unsqueeze(0))
 
         w_planes = keep.tile([P, K], U8, align_bytes=64)
         nc.vector.memset(w_planes[:].bitcast(I32), 0)
@@ -86,12 +88,12 @@ def tile_dsfs_pa_kernel(tc, x, feat_w, feat_b, trans_w_words, trans_w_scales, tr
         for r in range(4, ROW_BLOCKS):
             load_x(r)
 
-        def spread_bias(i):
-            bias_all = keep.tile([P, K], BF16, name="bias_all%d" % i)
+        def spread_bias(bias_row, name):
+            bias_all = keep.tile([P, K], BF16, name=name)
             for c in range(COLUMN_BLOCKS):
                 cols = slice(c * BANK, (c + 1) * BANK)
                 repeated = psum_sum.tile([P, BANK], F32, tag="sum")
-                nc.tensor.matmul(out=repeated[:], lhsT=ones[:], rhs=bias_rows[:, i, cols], start=True, stop=True)
+                nc.tensor.matmul(out=repeated[:], lhsT=ones[:], rhs=bias_row[:, cols], start=True, stop=True)
                 nc.vector.tensor_copy(out=bias_all[:, cols], in_=repeated[:])
             return bias_all
 
@@ -111,7 +113,7 @@ def tile_dsfs_pa_kernel(tc, x, feat_w, feat_b, trans_w_words, trans_w_scales, tr
             h_sorted = triple.tile([P, K], BF16)
             return h_f32, h_sorted
 
-        def feature_pass(g, x_t, feat_b_all, h_f32, h_sorted):
+        def feature_products(g, x_t, h_f32):
             cols = slice(g * K_PASS, (g + 1) * K_PASS)
             products = psum_sum.tile([P, K_PASS], F32, tag="sum")
             for j in range(FEATURES_PER_PASS):
@@ -120,6 +122,9 @@ def tile_dsfs_pa_kernel(tc, x, feat_w, feat_b, trans_w_words, trans_w_scales, tr
                     out=products[:, j * H : (j + 1) * H], lhsT=x_t[:, f, :], rhs=feat_w_sb[:, f, :], start=True, stop=True
                 )
             nc.vector.tensor_tensor(out=h_f32[:, cols], in0=products[:], in1=feat_b_all[:, cols], op=ADD)
+
+        def feature_round(g, h_f32, h_sorted):
+            cols = slice(g * K_PASS, (g + 1) * K_PASS)
             nc.scalar.activation(
                 out=h_sorted[:, cols].rearrange("b (u p e) -> b u p e", u=2, e=2),
                 in_=h_f32[:, cols].rearrange("b (p u e) -> b u p e", u=2, e=2),
@@ -185,34 +190,45 @@ def tile_dsfs_pa_kernel(tc, x, feat_w, feat_b, trans_w_words, trans_w_scales, tr
                 waiting = result
             finish(COLUMN_BLOCKS - 1, waiting)
 
+        first_half = range(PASSES // 2)
+        second_half = range(PASSES // 2, PASSES)
         turned_x = {}
         layers = {}
         quantised = {}
+
+        def small_layers_at_once(r):
+            layers[r] = feature_tiles()
+            for g in range(PASSES):
+                feature_products(g, turned_x[r], layers[r][0])
+                feature_round(g, *layers[r])
+
+        feat_b_all = spread_bias(feat_b_row, "feat_b_all")
         turned_x[0] = transpose_x(0)
-        feat_b_all = spread_bias(0)
         turned_x[1] = transpose_x(1)
-        layers[0] = feature_tiles()
-        for g in range(PASSES):
-            feature_pass(g, turned_x[0], feat_b_all, *layers[0])
+        small_layers_at_once(0)
         turned_x[2] = transpose_x(2)
-        layers[1] = feature_tiles()
-        for g in range(PASSES):
-            feature_pass(g, turned_x[1], feat_b_all, *layers[1])
-        trans_b_all = spread_bias(1)
+        small_layers_at_once(1)
+        trans_b_all = spread_bias(trans_b_row, "trans_b_all")
         quantised[0] = quantise_h(transpose_h(layers[0][1]))
         for r in range(ROW_BLOCKS):
             if r + 1 < ROW_BLOCKS:
                 grouped_next = transpose_h(layers[r + 1][1])
-            if r + 3 < ROW_BLOCKS:
-                turned_x[r + 3] = transpose_x(r + 3)
-            for g in range(PASSES // 2):
-                residual_relu(g, layers[r][0])
             if r + 2 < ROW_BLOCKS:
                 layers[r + 2] = feature_tiles()
-                for g in range(PASSES):
-                    feature_pass(g, turned_x[r + 2], feat_b_all, *layers[r + 2])
+                for g in first_half:
+                    feature_products(g, turned_x[r + 2], layers[r + 2][0])
+            if r + 3 < ROW_BLOCKS:
+                turned_x[r + 3] = transpose_x(r + 3)
+            for g in first_half:
+                residual_relu(g, layers[r][0])
+            if r + 2 < ROW_BLOCKS:
+                for g in first_half:
+                    feature_round(g, *layers[r + 2])
+                for g in second_half:
+                    feature_products(g, turned_x[r + 2], layers[r + 2][0])
+                    feature_round(g, *layers[r + 2])
             if r + 1 < ROW_BLOCKS:
                 quantised[r + 1] = quantise_h(grouped_next)
-            for g in range(PASSES // 2, PASSES):
+            for g in second_half:
                 residual_relu(g, layers[r][0])
             big_matmul(r, *quantised[r], layers[r][0], trans_b_all)

@@ -48,12 +48,11 @@ def tile_dsfs_pa_kernel(tc, x, feat_w, feat_b, trans_w_words, trans_w_scales, tr
 
         feat_b_row = keep.tile([P, K], BF16)
         nc.vector.memset(feat_b_row[:].bitcast(I32), 0)
-        nc.scalar.dma_start(out=feat_b_row[0:1, :], in_=feat_b.rearrange("f h -> (f h)").unsqueeze(0))
+        nc.sync.dma_start(out=feat_b_row[0:1, :], in_=feat_b.rearrange("f h -> (f h)").unsqueeze(0))
         ones = keep.tile([P, P], BF16)
         nc.vector.memset(ones[:], 1.0)
         trans_b_row = keep.tile([P, K], BF16)
         nc.vector.memset(trans_b_row[:].bitcast(I32), 0)
-        nc.scalar.dma_start(out=trans_b_row[0:1, :], in_=trans_b.unsqueeze(0))
 
         w_planes = keep.tile([P, K], U8, align_bytes=64)
         nc.vector.memset(w_planes[:].bitcast(I32), 0)
@@ -72,6 +71,7 @@ def tile_dsfs_pa_kernel(tc, x, feat_w, feat_b, trans_w_words, trans_w_scales, tr
             nc.sync.dma_start(out=w_words[:, :, some].bitcast(I32), in_=w_words_dram[:, :, some].bitcast(I32))
 
         load_x(0)
+        nc.sync.dma_start(out=trans_b_row[0:1, :], in_=trans_b.unsqueeze(0))
         nc.sync.dma_start(out=feat_w_sb[:], in_=feat_w.rearrange("f e h -> e f h"))
         load_x(1)
         load_x(2)

@@ -48,7 +48,6 @@ def tile_dsfs_pa_kernel(tc, x, feat_w, feat_b, trans_w_words, trans_w_scales, tr
 
         feat_b_row = keep.tile([P, K], BF16)
         nc.vector.memset(feat_b_row[:].bitcast(I32), 0)
-        nc.sync.dma_start(out=feat_b_row[0:1, :], in_=feat_b.rearrange("f h -> (f h)").unsqueeze(0))
         ones = keep.tile([P, P], BF16)
         nc.vector.memset(ones[:], 1.0)
         trans_b_row = keep.tile([P, K], BF16)
@@ -71,8 +70,9 @@ def tile_dsfs_pa_kernel(tc, x, feat_w, feat_b, trans_w_words, trans_w_scales, tr
             nc.sync.dma_start(out=w_words[:, :, some].bitcast(I32), in_=w_words_dram[:, :, some].bitcast(I32))
 
         load_x(0)
-        nc.sync.dma_start(out=trans_b_row[0:1, :], in_=trans_b.unsqueeze(0))
+        nc.sync.dma_start(out=feat_b_row[0:1, :], in_=feat_b.rearrange("f h -> (f h)").unsqueeze(0))
         nc.sync.dma_start(out=feat_w_sb[:], in_=feat_w.rearrange("f e h -> e f h"))
+        nc.sync.dma_start(out=trans_b_row[0:1, :], in_=trans_b.unsqueeze(0))
         load_x(1)
         load_x(2)
         for quadrant in range(P // QUADRANT):
@@ -159,36 +159,36 @@ def tile_dsfs_pa_kernel(tc, x, feat_w, feat_b, trans_w_words, trans_w_scales, tr
             h_plane = triple.tile([P, PASSES * P], U8, align_bytes=64)
             nc.vector.quantize_mx(out=h_codes[:].bitcast(FP8X4), scales=h_plane[:], in_=grouped[:])
             return h_codes, h_plane
+        unfinished = []
 
-        def big_matmul(r, h_codes, h_plane, h_f32, trans_b_all):
-            def finish(c, result):
+        def finish_older(keep_newest):
+            for block in list(unfinished[: len(unfinished) - keep_newest]):
+                unfinished.remove(block)
+                r, c, result, h_f32 = block
                 cols = slice(c * BANK, (c + 1) * BANK)
                 nc.vector.scalar_tensor_tensor(
                     out=result[:], in0=result[:], scalar=0.0, in1=h_f32[:, cols], op0=MAX, op1=ADD
                 )
                 nc.sync.dma_start(out=out[r * P : (r + 1) * P, cols], in_=result[:])
 
-            waiting = None
-            for c in range(COLUMN_BLOCKS):
-                cols = slice(c * BANK, (c + 1) * BANK)
-                sums = psum_sum.tile([P, BANK], F32, tag="sum")
-                for g in range(PASSES):
-                    rows_of_g = slice(g * P, (g + 1) * P)
-                    nc.tensor.matmul_mx(
-                        out=sums[:],
-                        lhsT=h_codes[:, rows_of_g].bitcast(FP8X4),
-                        lhsT_scale=h_plane[:, rows_of_g],
-                        rhs=w_words[:, g, c * BANK * PACK : (c + 1) * BANK * PACK].bitcast(FP8X4),
-                        rhs_scale=w_planes[g * PLANE_STEP : P, cols],
-                        start=(g == 0),
-                        stop=(g == PASSES - 1),
-                    )
-                result = results.tile([P, BANK], F32)
-                nc.vector.tensor_tensor(out=result[:], in0=sums[:], in1=trans_b_all[:, cols], op=ADD)
-                if waiting is not None:
-                    finish(c - 1, waiting)
-                waiting = result
-            finish(COLUMN_BLOCKS - 1, waiting)
+        def big_matmul(r, c, h_codes, h_plane, h_f32):
+            cols = slice(c * BANK, (c + 1) * BANK)
+            sums = psum_sum.tile([P, BANK], F32, tag="sum")
+            for g in range(PASSES):
+                rows_of_g = slice(g * P, (g + 1) * P)
+                nc.tensor.matmul_mx(
+                    out=sums[:],
+                    lhsT=h_codes[:, rows_of_g].bitcast(FP8X4),
+                    lhsT_scale=h_plane[:, rows_of_g],
+                    rhs=w_words[:, g, c * BANK * PACK : (c + 1) * BANK * PACK].bitcast(FP8X4),
+                    rhs_scale=w_planes[g * PLANE_STEP : P, cols],
+                    start=(g == 0),
+                    stop=(g == PASSES - 1),
+                )
+            result = results.tile([P, BANK], F32)
+            nc.vector.tensor_tensor(out=result[:], in0=sums[:], in1=trans_b_all[:, cols], op=ADD)
+            unfinished.append((r, c, result, h_f32))
+            finish_older(1)
 
         first_half = range(PASSES // 2)
         second_half = range(PASSES // 2, PASSES)
@@ -196,30 +196,36 @@ def tile_dsfs_pa_kernel(tc, x, feat_w, feat_b, trans_w_words, trans_w_scales, tr
         layers = {}
         quantised = {}
 
-        def small_layers_at_once(r):
-            layers[r] = feature_tiles()
-            for g in range(PASSES):
-                feature_products(g, turned_x[r], layers[r][0])
-                feature_round(g, *layers[r])
-
-        feat_b_all = spread_bias(feat_b_row, "feat_b_all")
         turned_x[0] = transpose_x(0)
+        feat_b_all = spread_bias(feat_b_row, "feat_b_all")
         turned_x[1] = transpose_x(1)
-        small_layers_at_once(0)
-        turned_x[2] = transpose_x(2)
-        small_layers_at_once(1)
-        trans_b_all = spread_bias(trans_b_row, "trans_b_all")
+        layers[0] = feature_tiles()
+        for g in range(PASSES):
+            feature_products(g, turned_x[0], layers[0][0])
+            feature_round(g, *layers[0])
+        layers[1] = feature_tiles()
+        for g in range(PASSES):
+            feature_products(g, turned_x[1], layers[1][0])
         quantised[0] = quantise_h(transpose_h(layers[0][1]))
+        for g in first_half:
+            residual_relu(g, layers[0][0])
+        trans_b_all = spread_bias(trans_b_row, "trans_b_all")
+        for g in range(PASSES):
+            feature_round(g, *layers[1])
+        turned_x[2] = transpose_x(2)
         for r in range(ROW_BLOCKS):
+            for c in first_half:
+                big_matmul(r, c, *quantised[r], layers[r][0])
             if r + 1 < ROW_BLOCKS:
                 grouped_next = transpose_h(layers[r + 1][1])
             if r + 2 < ROW_BLOCKS:
                 layers[r + 2] = feature_tiles()
                 for g in first_half:
                     feature_products(g, turned_x[r + 2], layers[r + 2][0])
+                    finish_older(0)
             if r + 3 < ROW_BLOCKS:
                 turned_x[r + 3] = transpose_x(r + 3)
-            for g in first_half:
+            for g in second_half:
                 residual_relu(g, layers[r][0])
             if r + 2 < ROW_BLOCKS:
                 for g in first_half:
@@ -229,6 +235,8 @@ def tile_dsfs_pa_kernel(tc, x, feat_w, feat_b, trans_w_words, trans_w_scales, tr
                     feature_round(g, *layers[r + 2])
             if r + 1 < ROW_BLOCKS:
                 quantised[r + 1] = quantise_h(grouped_next)
-            for g in second_half:
-                residual_relu(g, layers[r][0])
-            big_matmul(r, *quantised[r], layers[r][0], trans_b_all)
+                for g in first_half:
+                    residual_relu(g, layers[r + 1][0])
+            for c in second_half:
+                big_matmul(r, c, *quantised[r], layers[r][0])
+        finish_older(0)

@@ -25,6 +25,7 @@ COLUMN_BLOCKS = K // BANK
 ROW_BLOCKS = BATCH // P
 PLANE_STEP = 4
 QUADRANT = 32
+WARM_UP_MATMULS = 3
 
 FLOPS = 2 * BATCH * FEATURES * E * H + 2 * BATCH * K * K
 
@@ -46,12 +47,12 @@ def tile_dsfs_pa_kernel(tc, x, feat_w, feat_b, trans_w_words, trans_w_scales, tr
         ident_f32 = keep.tile([P, P], F32)
         make_identity(nc, ident_f32[:])
 
-        feat_b_row = keep.tile([P, K], BF16)
-        nc.vector.memset(feat_b_row[:].bitcast(I32), 0)
-        ones = keep.tile([P, P], BF16)
-        nc.vector.memset(ones[:], 1.0)
-        trans_b_row = keep.tile([P, K], BF16)
-        nc.vector.memset(trans_b_row[:].bitcast(I32), 0)
+        zeros = keep.tile([P, BANK], BF16)
+        nc.vector.memset(zeros[:].bitcast(I32), 0)
+
+        bias_rows = keep.tile([P, H], BF16)
+        nc.vector.memset(bias_rows[QUADRANT : 2 * QUADRANT, :].bitcast(I32), 0)
+        nc.vector.memset(bias_rows[2 * QUADRANT : P, :].bitcast(I32), 0)
 
         w_planes = keep.tile([P, K], U8, align_bytes=64)
         nc.vector.memset(w_planes[:].bitcast(I32), 0)
@@ -69,10 +70,11 @@ def tile_dsfs_pa_kernel(tc, x, feat_w, feat_b, trans_w_words, trans_w_scales, tr
             some = slice(c * BANK * PACK, (c + 1) * BANK * PACK)
             nc.sync.dma_start(out=w_words[:, :, some].bitcast(I32), in_=w_words_dram[:, :, some].bitcast(I32))
 
+        nc.sync.dma_start(out=bias_rows[0:FEATURES, :], in_=feat_b)
+        nc.sync.dma_start(out=bias_rows[FEATURES : 2 * FEATURES, :], in_=trans_b.rearrange("(f h) -> f h", h=H))
         load_x(0)
-        nc.sync.dma_start(out=feat_b_row[0:1, :], in_=feat_b.rearrange("f h -> (f h)").unsqueeze(0))
-        nc.sync.dma_start(out=feat_w_sb[:], in_=feat_w.rearrange("f e h -> e f h"))
-        nc.sync.dma_start(out=trans_b_row[0:1, :], in_=trans_b.unsqueeze(0))
+        for some in (slice(0, FEATURES // 2), slice(FEATURES // 2, FEATURES)):
+            nc.sync.dma_start(out=feat_w_sb[:, some, :], in_=feat_w[some].rearrange("f e h -> e f h"))
         load_x(1)
         load_x(2)
         for quadrant in range(P // QUADRANT):
@@ -88,16 +90,39 @@ def tile_dsfs_pa_kernel(tc, x, feat_w, feat_b, trans_w_words, trans_w_scales, tr
         for r in range(4, ROW_BLOCKS):
             load_x(r)
 
-        def spread_bias(bias_row, name):
+        def copy_words(on_vector, out, in_):
+            if on_vector:
+                nc.vector.tensor_copy(out=out, in_=in_)
+            else:
+                nc.scalar.copy(out=out, in_=in_)
+
+        def warm_up():
+            unread = psum_sum.tile([P, BANK], F32, tag="sum")
+            for i in range(WARM_UP_MATMULS):
+                nc.tensor.matmul(out=unread[:], lhsT=zeros[:, 0:P], rhs=zeros[:], start=True, stop=True)
+
+        def spread_bias(which, name, pool, tag):
             bias_all = keep.tile([P, K], BF16, name=name)
-            for c in range(COLUMN_BLOCKS):
-                cols = slice(c * BANK, (c + 1) * BANK)
-                repeated = psum_sum.tile([P, BANK], F32, tag="sum")
-                nc.tensor.matmul(out=repeated[:], lhsT=ones[:], rhs=bias_row[:, cols], start=True, stop=True)
-                nc.vector.tensor_copy(out=bias_all[:, cols], in_=repeated[:])
+            per_bank = 2 * BANK // H
+            for first in range(0, FEATURES, per_bank):
+                repeated = pool.tile([P, per_bank, H], BF16, tag=tag)
+                for j in range(per_bank):
+                    f = first + j
+                    nc.tensor.matmul(
+                        out=repeated[:, j, :],
+                        lhsT=ident_bf16[:, which * FEATURES + f : which * FEATURES + f + 1].to_broadcast([P, P]),
+                        rhs=bias_rows[:],
+                        start=True,
+                        stop=True,
+                    )
+                copy_words(
+                    True,
+                    bias_all[:, first * H : (first + per_bank) * H].bitcast(F32),
+                    repeated[:].rearrange("p f h -> p (f h)").bitcast(F32),
+                )
             return bias_all
 
-        def transpose_x(r):
+        def transpose_x(r, on_vector):
             x_t = triple.tile([E, FEATURES, P], BF16)
             per_bank = 2 * BANK // P
             for first in range(0, FEATURES, per_bank):
@@ -105,7 +130,11 @@ def tile_dsfs_pa_kernel(tc, x, feat_w, feat_b, trans_w_words, trans_w_scales, tr
                 for j in range(per_bank):
                     f = first + j
                     nc.tensor.transpose(out=turned[:, j, :], in_=x_blocks[r][:, f * E : (f + 1) * E], identity=ident_bf16[:])
-                nc.scalar.copy(out=x_t[:, first : first + per_bank, :], in_=turned[:])
+                copy_words(
+                    on_vector,
+                    x_t[:, first : first + per_bank, :].rearrange("e f b -> e (f b)").bitcast(F32),
+                    turned[:].rearrange("e f b -> e (f b)").bitcast(F32),
+                )
             return x_t
 
         def feature_tiles():
@@ -196,23 +225,27 @@ def tile_dsfs_pa_kernel(tc, x, feat_w, feat_b, trans_w_words, trans_w_scales, tr
         layers = {}
         quantised = {}
 
-        turned_x[0] = transpose_x(0)
-        feat_b_all = spread_bias(feat_b_row, "feat_b_all")
-        turned_x[1] = transpose_x(1)
+        warm_up()
+        feat_b_all = spread_bias(0, "feat_b_all", psum_t, "turned")
+        turned_x[0] = transpose_x(0, False)
         layers[0] = feature_tiles()
         for g in range(PASSES):
             feature_products(g, turned_x[0], layers[0][0])
             feature_round(g, *layers[0])
+        trans_b_all = spread_bias(1, "trans_b_all", psum_sum, "sum")
+        turned_x[1] = transpose_x(1, True)
+        grouped_first = transpose_h(layers[0][1])
         layers[1] = feature_tiles()
-        for g in range(PASSES):
+        for g in first_half:
             feature_products(g, turned_x[1], layers[1][0])
-        quantised[0] = quantise_h(transpose_h(layers[0][1]))
+        quantised[0] = quantise_h(grouped_first)
+        for g in second_half:
+            feature_products(g, turned_x[1], layers[1][0])
         for g in first_half:
             residual_relu(g, layers[0][0])
-        trans_b_all = spread_bias(trans_b_row, "trans_b_all")
         for g in range(PASSES):
             feature_round(g, *layers[1])
-        turned_x[2] = transpose_x(2)
+        turned_x[2] = transpose_x(2, False)
         for r in range(ROW_BLOCKS):
             for c in first_half:
                 big_matmul(r, c, *quantised[r], layers[r][0])
@@ -224,7 +257,7 @@ def tile_dsfs_pa_kernel(tc, x, feat_w, feat_b, trans_w_words, trans_w_scales, tr
                     feature_products(g, turned_x[r + 2], layers[r + 2][0])
                     finish_older(0)
             if r + 3 < ROW_BLOCKS:
-                turned_x[r + 3] = transpose_x(r + 3)
+                turned_x[r + 3] = transpose_x(r + 3, False)
             for g in second_half:
                 residual_relu(g, layers[r][0])
             if r + 2 < ROW_BLOCKS:

@@ -25,6 +25,7 @@ COLUMN_BLOCKS = K // BANK
 ROW_BLOCKS = BATCH // P
 PLANE_STEP = 4
 QUADRANT = 32
+TENSOR_BIAS_PASS = 3
 WARM_UP_MATMULS = 3
 
 FLOPS = 2 * BATCH * FEATURES * E * H + 2 * BATCH * K * K
@@ -142,27 +143,50 @@ def tile_dsfs_pa_kernel(tc, x, feat_w, feat_b, trans_w_words, trans_w_scales, tr
             h_sorted = triple.tile([P, K], BF16)
             return h_f32, h_sorted
 
+        biased_in_psum = {}
+
         def feature_products(g, x_t, h_f32):
             cols = slice(g * K_PASS, (g + 1) * K_PASS)
             products = psum_sum.tile([P, K_PASS], F32, tag="sum")
+            by_tensor = g == TENSOR_BIAS_PASS
             for j in range(FEATURES_PER_PASS):
                 f = g * FEATURES_PER_PASS + j
+                if by_tensor:
+                    nc.tensor.matmul(
+                        out=products[:, j * H : (j + 1) * H],
+                        lhsT=ident_bf16[:, f : f + 1].to_broadcast([P, P]),
+                        rhs=bias_rows[:],
+                        start=True,
+                        stop=False,
+                    )
                 nc.tensor.matmul(
-                    out=products[:, j * H : (j + 1) * H], lhsT=x_t[:, f, :], rhs=feat_w_sb[:, f, :], start=True, stop=True
+                    out=products[:, j * H : (j + 1) * H],
+                    lhsT=x_t[:, f, :],
+                    rhs=feat_w_sb[:, f, :],
+                    start=not by_tensor,
+                    stop=True,
                 )
-            nc.vector.tensor_tensor(out=h_f32[:, cols], in0=products[:], in1=feat_b_all[:, cols], op=ADD)
+            if by_tensor:
+                biased_in_psum[0] = products
+            else:
+                nc.vector.tensor_tensor(out=h_f32[:, cols], in0=products[:], in1=feat_b_all[:, cols], op=ADD)
 
         def feature_round(g, h_f32, h_sorted):
             cols = slice(g * K_PASS, (g + 1) * K_PASS)
+            by_tensor = g == TENSOR_BIAS_PASS
+            biased = biased_in_psum[0][:] if by_tensor else h_f32[:, cols]
             nc.scalar.activation(
                 out=h_sorted[:, cols].rearrange("b (u p e) -> b u p e", u=2, e=2),
-                in_=h_f32[:, cols].rearrange("b (p u e) -> b u p e", u=2, e=2),
+                in_=biased.rearrange("b (p u e) -> b u p e", u=2, e=2),
                 func=RELU,
             )
+            if by_tensor:
+                nc.scalar.activation(out=h_f32[:, cols], in_=biased, func=RELU)
 
         def residual_relu(g, h_f32):
             cols = slice(g * K_PASS, (g + 1) * K_PASS)
-            nc.scalar.activation(out=h_f32[:, cols], in_=h_f32[:, cols], func=RELU)
+            if g != TENSOR_BIAS_PASS:
+                nc.scalar.activation(out=h_f32[:, cols], in_=h_f32[:, cols], func=RELU)
 
         def transpose_h(h_sorted):
             h_words = h_sorted[:].bitcast(F32)

@@ -11,6 +11,7 @@ U8 = mybir.dt.uint8
 FP8X4 = mybir.dt.float8_e4m3fn_x4
 ADD = mybir.AluOpType.add
 MAX = mybir.AluOpType.max
+MULT = mybir.AluOpType.mult
 RELU = mybir.ActivationFunctionType.Relu
 
 P = 128
@@ -25,7 +26,8 @@ COLUMN_BLOCKS = K // BANK
 ROW_BLOCKS = BATCH // P
 PLANE_STEP = 4
 QUADRANT = 32
-TENSOR_BIAS_PASS = 3
+GPSIMD_BLOCK = 3
+TENSOR_BIAS_PASS = -1
 WARM_UP_MATMULS = 3
 
 FLOPS = 2 * BATCH * FEATURES * E * H + 2 * BATCH * K * K
@@ -239,9 +241,14 @@ def tile_dsfs_pa_kernel(tc, x, feat_w, feat_b, trans_w_words, trans_w_scales, tr
                     stop=(g == PASSES - 1),
                 )
             result = results.tile([P, BANK], F32)
-            nc.vector.tensor_tensor(out=result[:], in0=sums[:], in1=trans_b_all[:, cols], op=ADD)
-            unfinished.append((r, c, result, h_f32))
-            finish_older(1)
+            if c == GPSIMD_BLOCK and r < ROW_BLOCKS - 2:
+                nc.vector.tensor_tensor(out=result[:], in0=sums[:], in1=neg_trans_b[:], op=MAX)
+                nc.gpsimd.tensor_tensor(out=result[:], in0=result[:], in1=h_f32[:, cols], op=ADD)
+                nc.gpsimd.tensor_tensor(out=result[:], in0=result[:], in1=trans_b_all[:, cols], op=ADD)
+                nc.sync.dma_start(out=out[r * P : (r + 1) * P, cols], in_=result[:])
+            else:
+                nc.vector.tensor_tensor(out=result[:], in0=sums[:], in1=trans_b_all[:, cols], op=ADD)
+                unfinished.append((r, c, result, h_f32))
 
         first_half = range(PASSES // 2)
         second_half = range(PASSES // 2, PASSES)
@@ -257,6 +264,14 @@ def tile_dsfs_pa_kernel(tc, x, feat_w, feat_b, trans_w_words, trans_w_scales, tr
             feature_products(g, turned_x[0], layers[0][0])
             feature_round(g, *layers[0])
         trans_b_all = spread_bias(1, "trans_b_all", psum_sum, "sum")
+        neg_trans_b = keep.tile([P, BANK], BF16)
+        nc.vector.tensor_scalar(
+            out=neg_trans_b[:],
+            in0=trans_b_all[:, GPSIMD_BLOCK * BANK : (GPSIMD_BLOCK + 1) * BANK],
+            scalar1=-1.0,
+            scalar2=None,
+            op0=MULT,
+        )
         turned_x[1] = transpose_x(1, True)
         grouped_first = transpose_h(layers[0][1])
         layers[1] = feature_tiles()
@@ -279,7 +294,6 @@ def tile_dsfs_pa_kernel(tc, x, feat_w, feat_b, trans_w_words, trans_w_scales, tr
                 layers[r + 2] = feature_tiles()
                 for g in first_half:
                     feature_products(g, turned_x[r + 2], layers[r + 2][0])
-                    finish_older(0)
             if r + 3 < ROW_BLOCKS:
                 turned_x[r + 3] = transpose_x(r + 3, False)
             for g in second_half:
@@ -292,6 +306,8 @@ def tile_dsfs_pa_kernel(tc, x, feat_w, feat_b, trans_w_words, trans_w_scales, tr
                     feature_round(g, *layers[r + 2])
             if r + 1 < ROW_BLOCKS:
                 quantised[r + 1] = quantise_h(grouped_next)
+            finish_older(0)
+            if r + 1 < ROW_BLOCKS:
                 for g in first_half:
                     residual_relu(g, layers[r + 1][0])
             for c in second_half:

@@ -73,9 +73,9 @@ def tile_dsfs_pa_kernel(tc, x, feat_w, feat_b, trans_w_words, trans_w_scales, tr
             some = slice(c * BANK * PACK, (c + 1) * BANK * PACK)
             nc.sync.dma_start(out=w_words[:, :, some].bitcast(I32), in_=w_words_dram[:, :, some].bitcast(I32))
 
+        load_x(0)
         nc.sync.dma_start(out=bias_rows[0:FEATURES, :], in_=feat_b)
         nc.sync.dma_start(out=bias_rows[FEATURES : 2 * FEATURES, :], in_=trans_b.rearrange("(f h) -> f h", h=H))
-        load_x(0)
         for some in (slice(0, FEATURES // 2), slice(FEATURES // 2, FEATURES)):
             nc.sync.dma_start(out=feat_w_sb[:, some, :], in_=feat_w[some].rearrange("f e h -> e f h"))
         load_x(1)
@@ -257,8 +257,8 @@ def tile_dsfs_pa_kernel(tc, x, feat_w, feat_b, trans_w_words, trans_w_scales, tr
         quantised = {}
 
         warm_up()
-        feat_b_all = spread_bias(0, "feat_b_all", psum_t, "turned")
         turned_x[0] = transpose_x(0, False)
+        feat_b_all = spread_bias(0, "feat_b_all", psum_t, "turned")
         layers[0] = feature_tiles()
         for g in range(PASSES):
             feature_products(g, turned_x[0], layers[0][0])

@@ -57,13 +57,13 @@ def tile_dsfs_pa_kernel(tc, x, feat_w, feat_b, trans_w_words, trans_w_scales, tr
         nc.vector.memset(bias_rows[QUADRANT : 2 * QUADRANT, :].bitcast(I32), 0)
         nc.vector.memset(bias_rows[2 * QUADRANT : P, :].bitcast(I32), 0)
 
-        w_planes = keep.tile([P, K], U8, align_bytes=64)
+        w_planes = keep.tile([P, K], U8, align_bytes=256)
         nc.vector.memset(w_planes[:].bitcast(I32), 0)
 
         x_rows = x.rearrange("b f e -> b (f e)")
         x_blocks = [keep.tile([P, K], BF16, name="x_block%d" % r) for r in range(ROW_BLOCKS)]
         feat_w_sb = keep.tile([E, FEATURES, H], BF16)
-        w_words = keep.tile([P, PASSES, K * PACK], U8, align_bytes=64)
+        w_words = keep.tile([P, PASSES, K * PACK], U8, align_bytes=256)
         w_words_dram = trans_w_words.rearrange("g p n t -> p g (n t)")
 
         def load_x(r):
@@ -210,8 +210,8 @@ def tile_dsfs_pa_kernel(tc, x, feat_w, feat_b, trans_w_words, trans_w_scales, tr
             return grouped
 
         def quantise_h(grouped):
-            h_codes = triple.tile([P, PASSES * P], U32, align_bytes=64)
-            h_plane = triple.tile([P, PASSES * P], U8, align_bytes=64)
+            h_codes = triple.tile([P, PASSES * P], U32, align_bytes=256)
+            h_plane = triple.tile([P, PASSES * P], U8, align_bytes=256)
             nc.vector.quantize_mx(out=h_codes[:].bitcast(FP8X4), scales=h_plane[:], in_=grouped[:])
             return h_codes, h_plane
         unfinished = []

@@ -45,9 +45,9 @@ def tile_dsfs_pa_kernel(tc, x, feat_w, feat_b, trans_w_words, trans_w_scales, tr
         psum_sum = stack.enter_context(tc.psum_pool(name="psum_sum", bufs=4))
         stack.enter_context(tc.manual_schedule())
 
-        ident_bf16 = keep.tile([P, P], BF16)
+        ident_bf16 = keep.tile([P, P], BF16, align_bytes=256)
         make_identity(nc, ident_bf16[:])
-        ident_f32 = keep.tile([P, P], F32)
+        ident_f32 = keep.tile([P, P], F32, align_bytes=256)
         make_identity(nc, ident_f32[:])
 
         zeros = keep.tile([P, BANK], BF16)
@@ -61,8 +61,8 @@ def tile_dsfs_pa_kernel(tc, x, feat_w, feat_b, trans_w_words, trans_w_scales, tr
         nc.vector.memset(w_planes[:].bitcast(I32), 0)
 
         x_rows = x.rearrange("b f e -> b (f e)")
-        x_blocks = [keep.tile([P, K], BF16, name="x_block%d" % r) for r in range(ROW_BLOCKS)]
-        feat_w_sb = keep.tile([E, FEATURES, H], BF16)
+        x_blocks = [keep.tile([P, K], BF16, name="x_block%d" % r, align_bytes=256) for r in range(ROW_BLOCKS)]
+        feat_w_sb = keep.tile([E, FEATURES, H], BF16, align_bytes=256)
         w_words = keep.tile([P, PASSES, K * PACK], U8, align_bytes=256)
         w_words_dram = trans_w_words.rearrange("g p n t -> p g (n t)")
 
@@ -126,7 +126,7 @@ def tile_dsfs_pa_kernel(tc, x, feat_w, feat_b, trans_w_words, trans_w_scales, tr
             return bias_all
 
         def transpose_x(r, on_vector):
-            x_t = triple.tile([E, FEATURES, P], BF16)
+            x_t = triple.tile([E, FEATURES, P], BF16, align_bytes=256)
             per_bank = 2 * BANK // P
             for first in range(0, FEATURES, per_bank):
                 turned = psum_t.tile([E, per_bank, P], BF16, tag="turned")
@@ -142,7 +142,7 @@ def tile_dsfs_pa_kernel(tc, x, feat_w, feat_b, trans_w_words, trans_w_scales, tr
 
         def feature_tiles():
             h_f32 = quad.tile([P, K], F32)
-            h_sorted = triple.tile([P, K], BF16)
+            h_sorted = triple.tile([P, K], BF16, align_bytes=256)
             return h_f32, h_sorted
 
         biased_in_psum = {}

@@ -26,8 +26,30 @@ COLUMN_BLOCKS = K // BANK
 ROW_BLOCKS = BATCH // P
 PLANE_STEP = 4
 QUADRANT = 32
+PLANE_SLOT = 256
 GPSIMD_BLOCK = 3
-TENSOR_BIAS_PASS = -1
+LAST_BIAS = ()
+PAIR = True
+ROW0 = False
+MM1_EARLY = False
+X_LEAD = 3
+REL0 = (0, 1)
+GP_END = 2
+FIN_FIRST = 9
+PAIR_END = 8
+LATE_STORE = False
+LAST_NOW = False
+X2_WHEN = 0
+TB_WHEN = 0
+TB_DMA = True
+MM1_BEFORE = 2
+ADD_FIRST = True
+REL_LATE = True
+BEFORE_X = 3
+X1_BEFORE_TB = True
+X1_ENG = True
+FB_ENG = (True, False)
+TB_ENG = (False, False)
 WARM_UP_MATMULS = 3
 
 FLOPS = 2 * BATCH * FEATURES * E * H + 2 * BATCH * K * K
@@ -104,7 +126,7 @@ def tile_dsfs_pa_kernel(tc, x, feat_w, feat_b, trans_w_words, trans_w_scales, tr
             for i in range(WARM_UP_MATMULS):
                 nc.tensor.matmul(out=unread[:], lhsT=zeros[:, 0:P], rhs=zeros[:], start=True, stop=True)
 
-        def spread_bias(which, name, pool, tag):
+        def spread_bias(which, name, pool, tag, engines):
             bias_all = keep.tile([P, K], BF16, name=name)
             per_bank = 2 * BANK // H
             for first in range(0, FEATURES, per_bank):
@@ -119,23 +141,30 @@ def tile_dsfs_pa_kernel(tc, x, feat_w, feat_b, trans_w_words, trans_w_scales, tr
                         stop=True,
                     )
                 copy_words(
-                    True,
+                    engines[first // per_bank],
                     bias_all[:, first * H : (first + per_bank) * H].bitcast(F32),
                     repeated[:].rearrange("p f h -> p (f h)").bitcast(F32),
                 )
             return bias_all
 
         def transpose_x(r, on_vector):
-            x_t = triple.tile([E, FEATURES, P], BF16, align_bytes=256)
             per_bank = 2 * BANK // P
+            banks = []
             for first in range(0, FEATURES, per_bank):
                 turned = psum_t.tile([E, per_bank, P], BF16, tag="turned")
+                banks.append(turned)
                 for j in range(per_bank):
                     f = first + j
                     nc.tensor.transpose(out=turned[:, j, :], in_=x_blocks[r][:, f * E : (f + 1) * E], identity=ident_bf16[:])
+            return copy_x(banks, on_vector) if on_vector is not None else banks
+
+        def copy_x(banks, on_vector):
+            x_t = (quad if X_LEAD == 4 else triple).tile([E, FEATURES, P], BF16, align_bytes=256)
+            per_bank = 2 * BANK // P
+            for i, turned in enumerate(banks):
                 copy_words(
                     on_vector,
-                    x_t[:, first : first + per_bank, :].rearrange("e f b -> e (f b)").bitcast(F32),
+                    x_t[:, i * per_bank : (i + 1) * per_bank, :].rearrange("e f b -> e (f b)").bitcast(F32),
                     turned[:].rearrange("e f b -> e (f b)").bitcast(F32),
                 )
             return x_t
@@ -147,13 +176,16 @@ def tile_dsfs_pa_kernel(tc, x, feat_w, feat_b, trans_w_words, trans_w_scales, tr
 
         biased_in_psum = {}
 
-        def feature_products(g, x_t, h_f32):
+        def by_tensor(r, g):
+            return (r == 0 and ROW0) or (r == ROW_BLOCKS - 1 and g in LAST_BIAS)
+
+        def feature_products(g, r):
+            h_f32, h_sorted = layers[r]
             cols = slice(g * K_PASS, (g + 1) * K_PASS)
             products = psum_sum.tile([P, K_PASS], F32, tag="sum")
-            by_tensor = g == TENSOR_BIAS_PASS
             for j in range(FEATURES_PER_PASS):
                 f = g * FEATURES_PER_PASS + j
-                if by_tensor:
+                if by_tensor(r, g):
                     nc.tensor.matmul(
                         out=products[:, j * H : (j + 1) * H],
                         lhsT=ident_bf16[:, f : f + 1].to_broadcast([P, P]),
@@ -163,32 +195,41 @@ def tile_dsfs_pa_kernel(tc, x, feat_w, feat_b, trans_w_words, trans_w_scales, tr
                     )
                 nc.tensor.matmul(
                     out=products[:, j * H : (j + 1) * H],
-                    lhsT=x_t[:, f, :],
+                    lhsT=turned_x[r][:, f, :],
                     rhs=feat_w_sb[:, f, :],
-                    start=not by_tensor,
+                    start=not by_tensor(r, g),
                     stop=True,
                 )
-            if by_tensor:
-                biased_in_psum[0] = products
+            if by_tensor(r, g):
+                if r == 0:
+                    bf16_relu(g, r, products[:])
+                    nc.vector.tensor_scalar(out=h_f32[:, cols], in0=products[:], scalar1=0.0, scalar2=None, op0=MAX)
+                else:
+                    biased_in_psum[(r, g)] = products
             else:
                 nc.vector.tensor_tensor(out=h_f32[:, cols], in0=products[:], in1=feat_b_all[:, cols], op=ADD)
 
-        def feature_round(g, h_f32, h_sorted):
+        def bf16_relu(g, r, biased):
+            h_f32, h_sorted = layers[r]
             cols = slice(g * K_PASS, (g + 1) * K_PASS)
-            by_tensor = g == TENSOR_BIAS_PASS
-            biased = biased_in_psum[0][:] if by_tensor else h_f32[:, cols]
             nc.scalar.activation(
                 out=h_sorted[:, cols].rearrange("b (u p e) -> b u p e", u=2, e=2),
                 in_=biased.rearrange("b (p u e) -> b u p e", u=2, e=2),
                 func=RELU,
             )
-            if by_tensor:
-                nc.scalar.activation(out=h_f32[:, cols], in_=biased, func=RELU)
 
-        def residual_relu(g, h_f32):
+        def feature_round(g, r):
             cols = slice(g * K_PASS, (g + 1) * K_PASS)
-            if g != TENSOR_BIAS_PASS:
-                nc.scalar.activation(out=h_f32[:, cols], in_=h_f32[:, cols], func=RELU)
+            if not by_tensor(r, g):
+                bf16_relu(g, r, layers[r][0][:, cols])
+            elif r > 0:
+                bf16_relu(g, r, biased_in_psum[(r, g)][:])
+                nc.scalar.activation(out=layers[r][0][:, cols], in_=biased_in_psum[(r, g)][:], func=RELU)
+
+        def residual_relu(g, r):
+            cols = slice(g * K_PASS, (g + 1) * K_PASS)
+            if not by_tensor(r, g):
+                nc.scalar.activation(out=layers[r][0][:, cols], in_=layers[r][0][:, cols], func=RELU)
 
         def transpose_h(h_sorted):
             h_words = h_sorted[:].bitcast(F32)
@@ -211,22 +252,28 @@ def tile_dsfs_pa_kernel(tc, x, feat_w, feat_b, trans_w_words, trans_w_scales, tr
 
         def quantise_h(grouped):
             h_codes = triple.tile([P, PASSES * P], U32, align_bytes=256)
-            h_plane = triple.tile([P, PASSES * P], U8, align_bytes=256)
-            nc.vector.quantize_mx(out=h_codes[:].bitcast(FP8X4), scales=h_plane[:], in_=grouped[:])
+            h_plane = triple.tile([P, PASSES, PLANE_SLOT], U8, align_bytes=256)
+            for g in range(PASSES):
+                nc.vector.quantize_mx(
+                    out=h_codes[:, g * P : (g + 1) * P].bitcast(FP8X4),
+                    scales=h_plane[:, g, 0:P],
+                    in_=grouped[:, g * K_PASS : (g + 1) * K_PASS],
+                )
             return h_codes, h_plane
         unfinished = []
+        late_stores = []
+        wide_tiles = {}
 
         def finish_older(keep_newest):
             for block in list(unfinished[: len(unfinished) - keep_newest]):
                 unfinished.remove(block)
-                r, c, result, h_f32 = block
-                cols = slice(c * BANK, (c + 1) * BANK)
+                r, cols, result, h_f32 = block
                 nc.vector.scalar_tensor_tensor(
                     out=result[:], in0=result[:], scalar=0.0, in1=h_f32[:, cols], op0=MAX, op1=ADD
                 )
                 nc.sync.dma_start(out=out[r * P : (r + 1) * P, cols], in_=result[:])
 
-        def big_matmul(r, c, h_codes, h_plane, h_f32):
+        def mx_passes(r, c, h_codes, h_plane):
             cols = slice(c * BANK, (c + 1) * BANK)
             sums = psum_sum.tile([P, BANK], F32, tag="sum")
             for g in range(PASSES):
@@ -234,21 +281,38 @@ def tile_dsfs_pa_kernel(tc, x, feat_w, feat_b, trans_w_words, trans_w_scales, tr
                 nc.tensor.matmul_mx(
                     out=sums[:],
                     lhsT=h_codes[:, rows_of_g].bitcast(FP8X4),
-                    lhsT_scale=h_plane[:, rows_of_g],
+                    lhsT_scale=h_plane[:, g, 0:P],
                     rhs=w_words[:, g, c * BANK * PACK : (c + 1) * BANK * PACK].bitcast(FP8X4),
                     rhs_scale=w_planes[g * PLANE_STEP : P, cols],
                     start=(g == 0),
                     stop=(g == PASSES - 1),
                 )
+            return sums
+
+        def add_bias(r, c, sums, h_f32):
+            cols = slice(c * BANK, (c + 1) * BANK)
+            if PAIR and r < PAIR_END and c == 1:
+                wide = wide_tiles[0]
+                nc.vector.tensor_tensor(out=wide[:, BANK : 2 * BANK], in0=sums[:], in1=trans_b_all[:, cols], op=ADD)
+                unfinished.append((r, slice(0, 2 * BANK), wide, h_f32))
+                return
+            if PAIR and r < PAIR_END and c == 0:
+                wide = pair.tile([P, 2 * BANK], F32, name="wide")
+                wide_tiles[0] = wide
+                nc.vector.tensor_tensor(out=wide[:, 0:BANK], in0=sums[:], in1=trans_b_all[:, cols], op=ADD)
+                return
             result = results.tile([P, BANK], F32)
-            if c == GPSIMD_BLOCK and r < ROW_BLOCKS - 2:
+            if c == GPSIMD_BLOCK and r < ROW_BLOCKS - GP_END:
                 nc.vector.tensor_tensor(out=result[:], in0=sums[:], in1=neg_trans_b[:], op=MAX)
                 nc.gpsimd.tensor_tensor(out=result[:], in0=result[:], in1=h_f32[:, cols], op=ADD)
                 nc.gpsimd.tensor_tensor(out=result[:], in0=result[:], in1=trans_b_all[:, cols], op=ADD)
-                nc.sync.dma_start(out=out[r * P : (r + 1) * P, cols], in_=result[:])
+                if r >= ROW_BLOCKS - 2 and LATE_STORE:
+                    late_stores.append((r, cols, result))
+                else:
+                    nc.sync.dma_start(out=out[r * P : (r + 1) * P, cols], in_=result[:])
             else:
                 nc.vector.tensor_tensor(out=result[:], in0=sums[:], in1=trans_b_all[:, cols], op=ADD)
-                unfinished.append((r, c, result, h_f32))
+                unfinished.append((r, cols, result, h_f32))
 
         first_half = range(PASSES // 2)
         second_half = range(PASSES // 2, PASSES)
@@ -258,58 +322,73 @@ def tile_dsfs_pa_kernel(tc, x, feat_w, feat_b, trans_w_words, trans_w_scales, tr
 
         warm_up()
         turned_x[0] = transpose_x(0, False)
-        feat_b_all = spread_bias(0, "feat_b_all", psum_t, "turned")
+        feat_b_all = spread_bias(0, "feat_b_all", psum_t, "turned", FB_ENG)
         layers[0] = feature_tiles()
         for g in range(PASSES):
-            feature_products(g, turned_x[0], layers[0][0])
-            feature_round(g, *layers[0])
-        trans_b_all = spread_bias(1, "trans_b_all", psum_sum, "sum")
+            feature_products(g, 0)
+            feature_round(g, 0)
+        if X1_BEFORE_TB:
+            turned_x[1] = transpose_x(1, True)
+        trans_b_all = spread_bias(1, "trans_b_all", psum_sum, "sum", TB_ENG)
         neg_trans_b = keep.tile([P, BANK], BF16)
-        nc.vector.tensor_scalar(
-            out=neg_trans_b[:],
-            in0=trans_b_all[:, GPSIMD_BLOCK * BANK : (GPSIMD_BLOCK + 1) * BANK],
-            scalar1=-1.0,
-            scalar2=None,
-            op0=MULT,
-        )
-        turned_x[1] = transpose_x(1, True)
+        if not X1_BEFORE_TB:
+            turned_x[1] = transpose_x(1, True)
         grouped_first = transpose_h(layers[0][1])
         layers[1] = feature_tiles()
         for g in first_half:
-            feature_products(g, turned_x[1], layers[1][0])
+            feature_products(g, 1)
         quantised[0] = quantise_h(grouped_first)
         for g in second_half:
-            feature_products(g, turned_x[1], layers[1][0])
-        for g in first_half:
-            residual_relu(g, layers[0][0])
+            feature_products(g, 1)
         for g in range(PASSES):
-            feature_round(g, *layers[1])
+            feature_round(g, 1)
         turned_x[2] = transpose_x(2, False)
+        for g in first_half:
+            residual_relu(g, 0)
         for r in range(ROW_BLOCKS):
+            waiting = [mx_passes(r, c, *quantised[r]) for c in first_half]
             for c in first_half:
-                big_matmul(r, c, *quantised[r], layers[r][0])
+                add_bias(r, c, waiting[c], layers[r][0])
             if r + 1 < ROW_BLOCKS:
                 grouped_next = transpose_h(layers[r + 1][1])
             if r + 2 < ROW_BLOCKS:
                 layers[r + 2] = feature_tiles()
-                for g in first_half:
-                    feature_products(g, turned_x[r + 2], layers[r + 2][0])
-            if r + 3 < ROW_BLOCKS:
-                turned_x[r + 3] = transpose_x(r + 3, False)
-            for g in second_half:
-                residual_relu(g, layers[r][0])
-            if r + 2 < ROW_BLOCKS:
-                for g in first_half:
-                    feature_round(g, *layers[r + 2])
+                for g in range(BEFORE_X):
+                    feature_products(g, r + 2)
+            if r + X_LEAD < ROW_BLOCKS:
+                turned_x[r + X_LEAD] = transpose_x(r + X_LEAD, False)
+            if not REL_LATE:
                 for g in second_half:
-                    feature_products(g, turned_x[r + 2], layers[r + 2][0])
-                    feature_round(g, *layers[r + 2])
+                    residual_relu(g, r)
+            if r + 2 < ROW_BLOCKS:
+                for g in range(BEFORE_X):
+                    feature_round(g, r + 2)
+                for g in range(BEFORE_X, PASSES):
+                    feature_products(g, r + 2)
+                    feature_round(g, r + 2)
+            if REL_LATE:
+                for g in second_half:
+                    residual_relu(g, r)
+            if r >= FIN_FIRST:
+                finish_older(0)
             if r + 1 < ROW_BLOCKS:
                 quantised[r + 1] = quantise_h(grouped_next)
             finish_older(0)
             if r + 1 < ROW_BLOCKS:
                 for g in first_half:
-                    residual_relu(g, layers[r + 1][0])
+                    residual_relu(g, r + 1)
+            if r == 0:
+                nc.vector.tensor_scalar(
+                    out=neg_trans_b[:],
+                    in0=trans_b_all[:, GPSIMD_BLOCK * BANK : (GPSIMD_BLOCK + 1) * BANK],
+                    scalar1=-1.0,
+                    scalar2=None,
+                    op0=MULT,
+                )
             for c in second_half:
-                big_matmul(r, c, *quantised[r], layers[r][0])
+                add_bias(r, c, mx_passes(r, c, *quantised[r]), layers[r][0])
+                if r == ROW_BLOCKS - 1 and LAST_NOW:
+                    finish_older(0)
         finish_older(0)
+        for r, cols, result in late_stores:
+            nc.scalar.dma_start(out=out[r * P : (r + 1) * P, cols], in_=result[:])

@@ -45,6 +45,14 @@ TB_DMA = True
 MM1_BEFORE = 2
 ADD_FIRST = True
 REL_LATE = True
+DMA_ORDER = "x0 b f0 f1 x1 x2 p w0 w1 x3 w2 w3 x4 x5 x6 x7"
+X2_POS = 0
+XT_END = False
+C3_LATE = True
+BANKS_T = 4
+REL0_EARLY = True
+WEAVE = False
+TB_LATE = True
 BEFORE_X = 3
 X1_BEFORE_TB = True
 X1_ENG = True
@@ -63,8 +71,8 @@ def tile_dsfs_pa_kernel(tc, x, feat_w, feat_b, trans_w_words, trans_w_scales, tr
         triple = stack.enter_context(tc.tile_pool(name="triple", bufs=3))
         quad = stack.enter_context(tc.tile_pool(name="quad", bufs=4))
         results = stack.enter_context(tc.tile_pool(name="results", bufs=2 * COLUMN_BLOCKS))
-        psum_t = stack.enter_context(tc.psum_pool(name="psum_t", bufs=4))
-        psum_sum = stack.enter_context(tc.psum_pool(name="psum_sum", bufs=4))
+        psum_t = stack.enter_context(tc.psum_pool(name="psum_t", bufs=BANKS_T))
+        psum_sum = stack.enter_context(tc.psum_pool(name="psum_sum", bufs=8 - BANKS_T))
         stack.enter_context(tc.manual_schedule())
 
         ident_bf16 = keep.tile([P, P], BF16, align_bytes=256)
@@ -95,25 +103,39 @@ def tile_dsfs_pa_kernel(tc, x, feat_w, feat_b, trans_w_words, trans_w_scales, tr
             some = slice(c * BANK * PACK, (c + 1) * BANK * PACK)
             nc.sync.dma_start(out=w_words[:, :, some].bitcast(I32), in_=w_words_dram[:, :, some].bitcast(I32))
 
-        load_x(0)
-        nc.sync.dma_start(out=bias_rows[0:FEATURES, :], in_=feat_b)
-        nc.sync.dma_start(out=bias_rows[FEATURES : 2 * FEATURES, :], in_=trans_b.rearrange("(f h) -> f h", h=H))
-        for some in (slice(0, FEATURES // 2), slice(FEATURES // 2, FEATURES)):
+        def load_x0_half(i):
+            half = slice(i * K // 2, (i + 1) * K // 2)
+            nc.sync.dma_start(out=x_blocks[0][:, half], in_=x_rows[0:P, half])
+
+        def load_bias():
+            nc.sync.dma_start(out=bias_rows[0:FEATURES, :], in_=feat_b)
+            nc.sync.dma_start(out=bias_rows[FEATURES : 2 * FEATURES, :], in_=trans_b.rearrange("(f h) -> f h", h=H))
+
+        def load_feat_w(i):
+            some = slice(i * FEATURES // 2, (i + 1) * FEATURES // 2)
             nc.sync.dma_start(out=feat_w_sb[:, some, :], in_=feat_w[some].rearrange("f e h -> e f h"))
-        load_x(1)
-        load_x(2)
-        for quadrant in range(P // QUADRANT):
-            first = quadrant * QUADRANT
-            nc.sync.dma_start(
-                out=w_planes[first : first + PASSES * PLANE_STEP, :].bitcast(I32),
-                in_=trans_w_scales[:, 4 * quadrant : 4 * quadrant + 4, :].bitcast(I32),
-            )
-        load_w(0)
-        load_x(3)
-        for c in range(1, COLUMN_BLOCKS):
-            load_w(c)
-        for r in range(4, ROW_BLOCKS):
-            load_x(r)
+
+        def load_planes():
+            for quadrant in range(P // QUADRANT):
+                first = quadrant * QUADRANT
+                nc.sync.dma_start(
+                    out=w_planes[first : first + PASSES * PLANE_STEP, :].bitcast(I32),
+                    in_=trans_w_scales[:, 4 * quadrant : 4 * quadrant + 4, :].bitcast(I32),
+                )
+
+        for token in DMA_ORDER.split(" "):
+            if token == "b":
+                load_bias()
+            elif token == "p":
+                load_planes()
+            elif token in ("h0", "h1"):
+                load_x0_half(("h0", "h1").index(token))
+            elif token in ("f0", "f1"):
+                load_feat_w(("f0", "f1").index(token))
+            elif token in ("w0", "w1", "w2", "w3"):
+                load_w(("w0", "w1", "w2", "w3").index(token))
+            else:
+                load_x(("x0", "x1", "x2", "x3", "x4", "x5", "x6", "x7").index(token))
 
         def copy_words(on_vector, out, in_):
             if on_vector:
@@ -126,10 +148,9 @@ def tile_dsfs_pa_kernel(tc, x, feat_w, feat_b, trans_w_words, trans_w_scales, tr
             for i in range(WARM_UP_MATMULS):
                 nc.tensor.matmul(out=unread[:], lhsT=zeros[:, 0:P], rhs=zeros[:], start=True, stop=True)
 
-        def spread_bias(which, name, pool, tag, engines):
-            bias_all = keep.tile([P, K], BF16, name=name)
+        def spread_bias(which, bias_all, halves, pool, tag, engines):
             per_bank = 2 * BANK // H
-            for first in range(0, FEATURES, per_bank):
+            for first in [i * per_bank for i in halves]:
                 repeated = pool.tile([P, per_bank, H], BF16, tag=tag)
                 for j in range(per_bank):
                     f = first + j
@@ -145,7 +166,6 @@ def tile_dsfs_pa_kernel(tc, x, feat_w, feat_b, trans_w_words, trans_w_scales, tr
                     bias_all[:, first * H : (first + per_bank) * H].bitcast(F32),
                     repeated[:].rearrange("p f h -> p (f h)").bitcast(F32),
                 )
-            return bias_all
 
         def transpose_x(r, on_vector):
             per_bank = 2 * BANK // P
@@ -157,6 +177,18 @@ def tile_dsfs_pa_kernel(tc, x, feat_w, feat_b, trans_w_words, trans_w_scales, tr
                     f = first + j
                     nc.tensor.transpose(out=turned[:, j, :], in_=x_blocks[r][:, f * E : (f + 1) * E], identity=ident_bf16[:])
             return copy_x(banks, on_vector) if on_vector is not None else banks
+
+        def transpose_half(r, i, x_t):
+            per_bank = 2 * BANK // P
+            turned = psum_t.tile([E, per_bank, P], BF16, tag="turned")
+            for j in range(per_bank):
+                f = i * per_bank + j
+                nc.tensor.transpose(out=turned[:, j, :], in_=x_blocks[r][:, f * E : (f + 1) * E], identity=ident_bf16[:])
+            copy_words(
+                False,
+                x_t[:, i * per_bank : (i + 1) * per_bank, :].rearrange("e f b -> e (f b)").bitcast(F32),
+                turned[:].rearrange("e f b -> e (f b)").bitcast(F32),
+            )
 
         def copy_x(banks, on_vector):
             x_t = (quad if X_LEAD == 4 else triple).tile([E, FEATURES, P], BF16, align_bytes=256)
@@ -321,15 +353,23 @@ def tile_dsfs_pa_kernel(tc, x, feat_w, feat_b, trans_w_words, trans_w_scales, tr
         quantised = {}
 
         warm_up()
-        turned_x[0] = transpose_x(0, False)
-        feat_b_all = spread_bias(0, "feat_b_all", psum_t, "turned", FB_ENG)
+        feat_b_all = keep.tile([P, K], BF16, name="feat_b_all")
+        trans_b_all = keep.tile([P, K], BF16, name="trans_b_all")
+        if WEAVE:
+            turned_x[0] = (quad if X_LEAD == 4 else triple).tile([E, FEATURES, P], BF16, align_bytes=256, name="x_t0")
+            for i in range(2):
+                transpose_half(0, i, turned_x[0])
+                spread_bias(0, feat_b_all, (i,), psum_t, "turned", FB_ENG)
+        else:
+            turned_x[0] = transpose_x(0, False)
+            spread_bias(0, feat_b_all, (0, 1), psum_t, "turned", FB_ENG)
         layers[0] = feature_tiles()
         for g in range(PASSES):
             feature_products(g, 0)
             feature_round(g, 0)
         if X1_BEFORE_TB:
             turned_x[1] = transpose_x(1, True)
-        trans_b_all = spread_bias(1, "trans_b_all", psum_sum, "sum", TB_ENG)
+        spread_bias(1, trans_b_all, (0, 1), psum_sum, "sum", TB_ENG)
         neg_trans_b = keep.tile([P, BANK], BF16)
         if not X1_BEFORE_TB:
             turned_x[1] = transpose_x(1, True)
@@ -342,20 +382,28 @@ def tile_dsfs_pa_kernel(tc, x, feat_w, feat_b, trans_w_words, trans_w_scales, tr
             feature_products(g, 1)
         for g in range(PASSES):
             feature_round(g, 1)
-        turned_x[2] = transpose_x(2, False)
-        for g in first_half:
-            residual_relu(g, 0)
+        if X2_POS == 0:
+            turned_x[2] = transpose_x(2, False)
+        if REL0_EARLY:
+            for g in first_half:
+                residual_relu(g, 0)
         for r in range(ROW_BLOCKS):
-            waiting = [mx_passes(r, c, *quantised[r]) for c in first_half]
             for c in first_half:
-                add_bias(r, c, waiting[c], layers[r][0])
+                add_bias(r, c, mx_passes(r, c, *quantised[r]), layers[r][0])
+                if r == 0 and c + 1 == X2_POS:
+                    turned_x[2] = transpose_x(2, False)
+            if r == 1 and C3_LATE:
+                add_bias(0, 3, mx_passes(0, 3, *quantised[0]), layers[0][0])
+            if r == 0 and not REL0_EARLY:
+                for g in first_half:
+                    residual_relu(g, 0)
             if r + 1 < ROW_BLOCKS:
                 grouped_next = transpose_h(layers[r + 1][1])
             if r + 2 < ROW_BLOCKS:
                 layers[r + 2] = feature_tiles()
                 for g in range(BEFORE_X):
                     feature_products(g, r + 2)
-            if r + X_LEAD < ROW_BLOCKS:
+            if r + X_LEAD < ROW_BLOCKS and not XT_END:
                 turned_x[r + X_LEAD] = transpose_x(r + X_LEAD, False)
             if not REL_LATE:
                 for g in second_half:
@@ -386,9 +434,13 @@ def tile_dsfs_pa_kernel(tc, x, feat_w, feat_b, trans_w_words, trans_w_scales, tr
                     op0=MULT,
                 )
             for c in second_half:
+                if r == 0 and c == 3 and C3_LATE:
+                    continue
                 add_bias(r, c, mx_passes(r, c, *quantised[r]), layers[r][0])
                 if r == ROW_BLOCKS - 1 and LAST_NOW:
                     finish_older(0)
+            if r + X_LEAD < ROW_BLOCKS and XT_END:
+                turned_x[r + X_LEAD] = transpose_x(r + X_LEAD, False)
         finish_older(0)
         for r, cols, result in late_stores:
             nc.scalar.dma_start(out=out[r * P : (r + 1) * P, cols], in_=result[:])

from contextlib import ExitStack

import concourse.mybir as mybir
from concourse.masks import make_identity

BF16 = mybir.dt.bfloat16
F32 = mybir.dt.float32
I32 = mybir.dt.int32
U32 = mybir.dt.uint32
U8 = mybir.dt.uint8
FP8X4 = mybir.dt.float8_e4m3fn_x4
ADD = mybir.AluOpType.add
MAX = mybir.AluOpType.max
MULT = mybir.AluOpType.mult
RELU = mybir.ActivationFunctionType.Relu

P = 128
BATCH, FEATURES, E, H = 1024, 16, 128, 128
K = FEATURES * H
PACK = 4
K_PASS = P * PACK
PASSES = K // K_PASS
FEATURES_PER_PASS = K_PASS // H
BANK = 512
COLUMN_BLOCKS = K // BANK
ROW_BLOCKS = BATCH // P
PLANE_STEP = 4
QUADRANT = 32
PLANE_SLOT = 256
GPSIMD_BLOCK = 3
LAST_BIAS = ()
PAIR = True
ROW0 = False
MM1_EARLY = False
X_LEAD = 3
REL0 = (0, 1)
GP_END = 2
FIN_FIRST = 9
PAIR_END = 8
LATE_STORE = False
LAST_NOW = False
X2_WHEN = 0
TB_WHEN = 0
TB_DMA = True
MM1_BEFORE = 2
ADD_FIRST = True
REL_LATE = True
DMA_ORDER = "x0 b f0 f1 x1 x2 p w0 w1 x3 w2 w3 x4 x5 x6 x7"
X2_POS = 0
XT_END = False
C3_LATE = True
BANKS_T = 4
REL0_EARLY = True
WEAVE = False
TB_LATE = True
BEFORE_X = 3
X1_BEFORE_TB = True
X1_ENG = True
FB_ENG = (True, False)
TB_ENG = (False, False)
WARM_UP_MATMULS = 3

FLOPS = 2 * BATCH * FEATURES * E * H + 2 * BATCH * K * K


def tile_dsfs_pa_kernel(tc, x, feat_w, feat_b, trans_w_words, trans_w_scales, trans_b, out):
    nc = tc.nc
    with ExitStack() as stack:
        keep = stack.enter_context(tc.tile_pool(name="keep", bufs=1))
        pair = stack.enter_context(tc.tile_pool(name="pair", bufs=2))
        triple = stack.enter_context(tc.tile_pool(name="triple", bufs=3))
        quad = stack.enter_context(tc.tile_pool(name="quad", bufs=4))
        results = stack.enter_context(tc.tile_pool(name="results", bufs=2 * COLUMN_BLOCKS))
        psum_t = stack.enter_context(tc.psum_pool(name="psum_t", bufs=BANKS_T))
        psum_sum = stack.enter_context(tc.psum_pool(name="psum_sum", bufs=8 - BANKS_T))
        stack.enter_context(tc.manual_schedule())

        ident_bf16 = keep.tile([P, P], BF16, align_bytes=256)
        make_identity(nc, ident_bf16[:])
        ident_f32 = keep.tile([P, P], F32, align_bytes=256)
        make_identity(nc, ident_f32[:])

        zeros = keep.tile([P, BANK], BF16)
        nc.vector.memset(zeros[:].bitcast(I32), 0)

        bias_rows = keep.tile([P, H], BF16)
        nc.vector.memset(bias_rows[QUADRANT : 2 * QUADRANT, :].bitcast(I32), 0)
        nc.vector.memset(bias_rows[2 * QUADRANT : P, :].bitcast(I32), 0)

        w_planes = keep.tile([P, K], U8, align_bytes=256)
        nc.vector.memset(w_planes[:].bitcast(I32), 0)

        x_rows = x.rearrange("b f e -> b (f e)")
        x_blocks = [keep.tile([P, K], BF16, name="x_block%d" % r, align_bytes=256) for r in range(ROW_BLOCKS)]
        feat_w_sb = keep.tile([E, FEATURES, H], BF16, align_bytes=256)
        w_words = keep.tile([P, PASSES, K * PACK], U8, align_bytes=256)
        w_words_dram = trans_w_words.rearrange("g p n t -> p g (n t)")

        def load_x(r):
            nc.sync.dma_start(out=x_blocks[r][:], in_=x_rows[r * P : (r + 1) * P, :])

        def load_w(c):
            some = slice(c * BANK * PACK, (c + 1) * BANK * PACK)
            nc.sync.dma_start(out=w_words[:, :, some].bitcast(I32), in_=w_words_dram[:, :, some].bitcast(I32))

        def load_x0_half(i):
            half = slice(i * K // 2, (i + 1) * K // 2)
            nc.sync.dma_start(out=x_blocks[0][:, half], in_=x_rows[0:P, half])

        def load_bias():
            nc.sync.dma_start(out=bias_rows[0:FEATURES, :], in_=feat_b)
            nc.sync.dma_start(out=bias_rows[FEATURES : 2 * FEATURES, :], in_=trans_b.rearrange("(f h) -> f h", h=H))

        def load_feat_w(i):
            some = slice(i * FEATURES // 2, (i + 1) * FEATURES // 2)
            nc.sync.dma_start(out=feat_w_sb[:, some, :], in_=feat_w[some].rearrange("f e h -> e f h"))

        def load_planes():
            for quadrant in range(P // QUADRANT):
                first = quadrant * QUADRANT
                nc.sync.dma_start(
                    out=w_planes[first : first + PASSES * PLANE_STEP, :].bitcast(I32),
                    in_=trans_w_scales[:, 4 * quadrant : 4 * quadrant + 4, :].bitcast(I32),
                )

        for token in DMA_ORDER.split(" "):
            if token == "b":
                load_bias()
            elif token == "p":
                load_planes()
            elif token in ("h0", "h1"):
                load_x0_half(("h0", "h1").index(token))
            elif token in ("f0", "f1"):
                load_feat_w(("f0", "f1").index(token))
            elif token in ("w0", "w1", "w2", "w3"):
                load_w(("w0", "w1", "w2", "w3").index(token))
            else:
                load_x(("x0", "x1", "x2", "x3", "x4", "x5", "x6", "x7").index(token))

        def copy_words(on_vector, out, in_):
            if on_vector:
                nc.vector.tensor_copy(out=out, in_=in_)
            else:
                nc.scalar.copy(out=out, in_=in_)

        def warm_up():
            unread = psum_sum.tile([P, BANK], F32, tag="sum")
            for i in range(WARM_UP_MATMULS):
                nc.tensor.matmul(out=unread[:], lhsT=zeros[:, 0:P], rhs=zeros[:], start=True, stop=True)

        def spread_bias(which, bias_all, halves, pool, tag, engines):
            per_bank = 2 * BANK // H
            for first in [i * per_bank for i in halves]:
                repeated = pool.tile([P, per_bank, H], BF16, tag=tag)
                for j in range(per_bank):
                    f = first + j
                    nc.tensor.matmul(
                        out=repeated[:, j, :],
                        lhsT=ident_bf16[:, which * FEATURES + f : which * FEATURES + f + 1].to_broadcast([P, P]),
                        rhs=bias_rows[:],
                        start=True,
                        stop=True,
                    )
                copy_words(
                    engines[first // per_bank],
                    bias_all[:, first * H : (first + per_bank) * H].bitcast(F32),
                    repeated[:].rearrange("p f h -> p (f h)").bitcast(F32),
                )

        def transpose_x(r, on_vector):
            per_bank = 2 * BANK // P
            banks = []
            for first in range(0, FEATURES, per_bank):
                turned = psum_t.tile([E, per_bank, P], BF16, tag="turned")
                banks.append(turned)
                for j in range(per_bank):
                    f = first + j
                    nc.tensor.transpose(out=turned[:, j, :], in_=x_blocks[r][:, f * E : (f + 1) * E], identity=ident_bf16[:])
            return copy_x(banks, on_vector) if on_vector is not None else banks

        def transpose_half(r, i, x_t):
            per_bank = 2 * BANK // P
            turned = psum_t.tile([E, per_bank, P], BF16, tag="turned")
            for j in range(per_bank):
                f = i * per_bank + j
                nc.tensor.transpose(out=turned[:, j, :], in_=x_blocks[r][:, f * E : (f + 1) * E], identity=ident_bf16[:])
            copy_words(
                False,
                x_t[:, i * per_bank : (i + 1) * per_bank, :].rearrange("e f b -> e (f b)").bitcast(F32),
                turned[:].rearrange("e f b -> e (f b)").bitcast(F32),
            )

        def copy_x(banks, on_vector):
            x_t = (quad if X_LEAD == 4 else triple).tile([E, FEATURES, P], BF16, align_bytes=256)
            per_bank = 2 * BANK // P
            for i, turned in enumerate(banks):
                copy_words(
                    on_vector,
                    x_t[:, i * per_bank : (i + 1) * per_bank, :].rearrange("e f b -> e (f b)").bitcast(F32),
                    turned[:].rearrange("e f b -> e (f b)").bitcast(F32),
                )
            return x_t

        def feature_tiles():
            h_f32 = quad.tile([P, K], F32)
            h_sorted = triple.tile([P, K], BF16, align_bytes=256)
            return h_f32, h_sorted

        biased_in_psum = {}

        def by_tensor(r, g):
            return (r == 0 and ROW0) or (r == ROW_BLOCKS - 1 and g in LAST_BIAS)

        def feature_products(g, r):
            h_f32, h_sorted = layers[r]
            cols = slice(g * K_PASS, (g + 1) * K_PASS)
            products = psum_sum.tile([P, K_PASS], F32, tag="sum")
            for j in range(FEATURES_PER_PASS):
                f = g * FEATURES_PER_PASS + j
                if by_tensor(r, g):
                    nc.tensor.matmul(
                        out=products[:, j * H : (j + 1) * H],
                        lhsT=ident_bf16[:, f : f + 1].to_broadcast([P, P]),
                        rhs=bias_rows[:],
                        start=True,
                        stop=False,
                    )
                nc.tensor.matmul(
                    out=products[:, j * H : (j + 1) * H],
                    lhsT=turned_x[r][:, f, :],
                    rhs=feat_w_sb[:, f, :],
                    start=not by_tensor(r, g),
                    stop=True,
                )
            if by_tensor(r, g):
                if r == 0:
                    bf16_relu(g, r, products[:])
                    nc.vector.tensor_scalar(out=h_f32[:, cols], in0=products[:], scalar1=0.0, scalar2=None, op0=MAX)
                else:
                    biased_in_psum[(r, g)] = products
            else:
                nc.vector.tensor_tensor(out=h_f32[:, cols], in0=products[:], in1=feat_b_all[:, cols], op=ADD)

        def bf16_relu(g, r, biased):
            h_f32, h_sorted = layers[r]
            cols = slice(g * K_PASS, (g + 1) * K_PASS)
            nc.scalar.activation(
                out=h_sorted[:, cols].rearrange("b (u p e) -> b u p e", u=2, e=2),
                in_=biased.rearrange("b (p u e) -> b u p e", u=2, e=2),
                func=RELU,
            )

        def feature_round(g, r):
            cols = slice(g * K_PASS, (g + 1) * K_PASS)
            if not by_tensor(r, g):
                bf16_relu(g, r, layers[r][0][:, cols])
            elif r > 0:
                bf16_relu(g, r, biased_in_psum[(r, g)][:])
                nc.scalar.activation(out=layers[r][0][:, cols], in_=biased_in_psum[(r, g)][:], func=RELU)

        def residual_relu(g, r):
            cols = slice(g * K_PASS, (g + 1) * K_PASS)
            if not by_tensor(r, g):
                nc.scalar.activation(out=layers[r][0][:, cols], in_=layers[r][0][:, cols], func=RELU)

        def transpose_h(h_sorted):
            h_words = h_sorted[:].bitcast(F32)
            grouped = pair.tile([P, K], BF16, align_bytes=64)
            grouped_words = grouped[:].bitcast(F32)
            per_bank = BANK // (2 * P)
            for first in range(0, PASSES, per_bank):
                turned = psum_t.tile([P, per_bank, 2, P], F32, tag="turned")
                for j in range(per_bank):
                    for u in range(2):
                        start = ((first + j) * 2 + u) * P
                        nc.tensor.transpose(out=turned[:, j, u, :], in_=h_words[:, start : start + P], identity=ident_f32[:])
                nc.scalar.copy(
                    out=grouped_words[:, first * 2 * P : (first + per_bank) * 2 * P].rearrange(
                        "p (g b u) -> p g b u", g=per_bank, u=2
                    ),
                    in_=turned[:].rearrange("p g u b -> p g b u"),
                )
            return grouped

        def quantise_h(grouped):
            h_codes = triple.tile([P, PASSES * P], U32, align_bytes=256)
            h_plane = triple.tile([P, PASSES, PLANE_SLOT], U8, align_bytes=256)
            for g in range(PASSES):
                nc.vector.quantize_mx(
                    out=h_codes[:, g * P : (g + 1) * P].bitcast(FP8X4),
                    scales=h_plane[:, g, 0:P],
                    in_=grouped[:, g * K_PASS : (g + 1) * K_PASS],
                )
            return h_codes, h_plane
        unfinished = []
        late_stores = []
        wide_tiles = {}

        def finish_older(keep_newest):
            for block in list(unfinished[: len(unfinished) - keep_newest]):
                unfinished.remove(block)
                r, cols, result, h_f32 = block
                nc.vector.scalar_tensor_tensor(
                    out=result[:], in0=result[:], scalar=0.0, in1=h_f32[:, cols], op0=MAX, op1=ADD
                )
                nc.sync.dma_start(out=out[r * P : (r + 1) * P, cols], in_=result[:])

        def mx_passes(r, c, h_codes, h_plane):
            cols = slice(c * BANK, (c + 1) * BANK)
            sums = psum_sum.tile([P, BANK], F32, tag="sum")
            for g in range(PASSES):
                rows_of_g = slice(g * P, (g + 1) * P)
                nc.tensor.matmul_mx(
                    out=sums[:],
                    lhsT=h_codes[:, rows_of_g].bitcast(FP8X4),
                    lhsT_scale=h_plane[:, g, 0:P],
                    rhs=w_words[:, g, c * BANK * PACK : (c + 1) * BANK * PACK].bitcast(FP8X4),
                    rhs_scale=w_planes[g * PLANE_STEP : P, cols],
                    start=(g == 0),
                    stop=(g == PASSES - 1),
                )
            return sums

        def add_bias(r, c, sums, h_f32):
            cols = slice(c * BANK, (c + 1) * BANK)
            if PAIR and r < PAIR_END and c == 1:
                wide = wide_tiles[0]
                nc.vector.tensor_tensor(out=wide[:, BANK : 2 * BANK], in0=sums[:], in1=trans_b_all[:, cols], op=ADD)
                unfinished.append((r, slice(0, 2 * BANK), wide, h_f32))
                return
            if PAIR and r < PAIR_END and c == 0:
                wide = pair.tile([P, 2 * BANK], F32, name="wide")
                wide_tiles[0] = wide
                nc.vector.tensor_tensor(out=wide[:, 0:BANK], in0=sums[:], in1=trans_b_all[:, cols], op=ADD)
                return
            result = results.tile([P, BANK], F32)
            if c == GPSIMD_BLOCK and r < ROW_BLOCKS - GP_END:
                nc.vector.tensor_tensor(out=result[:], in0=sums[:], in1=neg_trans_b[:], op=MAX)
                nc.gpsimd.tensor_tensor(out=result[:], in0=result[:], in1=h_f32[:, cols], op=ADD)
                nc.gpsimd.tensor_tensor(out=result[:], in0=result[:], in1=trans_b_all[:, cols], op=ADD)
                if r >= ROW_BLOCKS - 2 and LATE_STORE:
                    late_stores.append((r, cols, result))
                else:
                    nc.sync.dma_start(out=out[r * P : (r + 1) * P, cols], in_=result[:])
            else:
                nc.vector.tensor_tensor(out=result[:], in0=sums[:], in1=trans_b_all[:, cols], op=ADD)
                unfinished.append((r, cols, result, h_f32))

        first_half = range(PASSES // 2)
        second_half = range(PASSES // 2, PASSES)
        turned_x = {}
        layers = {}
        quantised = {}

        warm_up()
        feat_b_all = keep.tile([P, K], BF16, name="feat_b_all")
        trans_b_all = keep.tile([P, K], BF16, name="trans_b_all")
        if WEAVE:
            turned_x[0] = (quad if X_LEAD == 4 else triple).tile([E, FEATURES, P], BF16, align_bytes=256, name="x_t0")
            for i in range(2):
                transpose_half(0, i, turned_x[0])
                spread_bias(0, feat_b_all, (i,), psum_t, "turned", FB_ENG)
        else:
            turned_x[0] = transpose_x(0, False)
            spread_bias(0, feat_b_all, (0, 1), psum_t, "turned", FB_ENG)
        layers[0] = feature_tiles()
        for g in range(PASSES):
            feature_products(g, 0)
            feature_round(g, 0)
        if X1_BEFORE_TB:
            turned_x[1] = transpose_x(1, True)
        spread_bias(1, trans_b_all, (0, 1), psum_sum, "sum", TB_ENG)
        neg_trans_b = keep.tile([P, BANK], BF16)
        if not X1_BEFORE_TB:
            turned_x[1] = transpose_x(1, True)
        grouped_first = transpose_h(layers[0][1])
        layers[1] = feature_tiles()
        for g in first_half:
            feature_products(g, 1)
        quantised[0] = quantise_h(grouped_first)
        for g in second_half:
            feature_products(g, 1)
        for g in range(PASSES):
            feature_round(g, 1)
        if X2_POS == 0:
            turned_x[2] = transpose_x(2, False)
        if REL0_EARLY:
            for g in first_half:
                residual_relu(g, 0)
        for r in range(ROW_BLOCKS):
            for c in first_half:
                add_bias(r, c, mx_passes(r, c, *quantised[r]), layers[r][0])
                if r == 0 and c + 1 == X2_POS:
                    turned_x[2] = transpose_x(2, False)
            if r == 1 and C3_LATE:
                add_bias(0, 3, mx_passes(0, 3, *quantised[0]), layers[0][0])
            if r == 0 and not REL0_EARLY:
                for g in first_half:
                    residual_relu(g, 0)
            if r + 1 < ROW_BLOCKS:
                grouped_next = transpose_h(layers[r + 1][1])
            if r + 2 < ROW_BLOCKS:
                layers[r + 2] = feature_tiles()
                for g in range(BEFORE_X):
                    feature_products(g, r + 2)
            if r + X_LEAD < ROW_BLOCKS and not XT_END:
                turned_x[r + X_LEAD] = transpose_x(r + X_LEAD, False)
            if not REL_LATE:
                for g in second_half:
                    residual_relu(g, r)
            if r + 2 < ROW_BLOCKS:
                for g in range(BEFORE_X):
                    feature_round(g, r + 2)
                for g in range(BEFORE_X, PASSES):
                    feature_products(g, r + 2)
                    feature_round(g, r + 2)
            if REL_LATE:
                for g in second_half:
                    residual_relu(g, r)
            if r >= FIN_FIRST:
                finish_older(0)
            if r + 1 < ROW_BLOCKS:
                quantised[r + 1] = quantise_h(grouped_next)
            finish_older(0)
            if r + 1 < ROW_BLOCKS:
                for g in first_half:
                    residual_relu(g, r + 1)
            if r == 0:
                nc.vector.tensor_scalar(
                    out=neg_trans_b[:],
                    in0=trans_b_all[:, GPSIMD_BLOCK * BANK : (GPSIMD_BLOCK + 1) * BANK],
                    scalar1=-1.0,
                    scalar2=None,
                    op0=MULT,
                )
            for c in second_half:
                if r == 0 and c == 3 and C3_LATE:
                    continue
                add_bias(r, c, mx_passes(r, c, *quantised[r]), layers[r][0])
                if r == ROW_BLOCKS - 1 and LAST_NOW:
                    finish_older(0)
            if r + X_LEAD < ROW_BLOCKS and XT_END:
                turned_x[r + X_LEAD] = transpose_x(r + X_LEAD, False)
        finish_older(0)
        for r, cols, result in late_stores:
            nc.scalar.dma_start(out=out[r * P : (r + 1) * P, cols], in_=result[:])
